import numpy as np
import ml_dtypes


def mxq(x, axis, fmt="e4m3"):
    dtype, down = {"e4m3": (ml_dtypes.float8_e4m3fn, 7), "e5m2": (ml_dtypes.float8_e5m2, 14)}[fmt]
    v = np.moveaxis(np.asarray(x, np.float32).astype(ml_dtypes.bfloat16).astype(np.float64), axis, -1)
    blocks = v.reshape(v.shape[:-1] + (-1, 32))
    amax = np.abs(blocks).max(-1, keepdims=True)
    byte = np.maximum(np.where(amax > 0, np.frexp(amax)[1] - 1 + 127, 0) - down, 1)
    scale = np.exp2(byte - 127.0)
    codes = (blocks / scale).astype(np.float32).astype(dtype).astype(np.float64)
    return np.moveaxis((codes * scale).reshape(v.shape), -1, axis)


WIDE = False


def mx_kscale(k):
    if not WIDE:
        return np.ones(k)
    levels = np.array([20, -20, 10, -10, 0])
    a = np.random.permutation(np.resize(levels, k // 512 * 4)).reshape(k // 512, 4)
    idx = np.arange(k)
    return np.exp2(a[idx // 512, idx % 128 // 32])


BF16 = ml_dtypes.bfloat16


def bf(x):
    return np.asarray(x, np.float32).astype(BF16)


def f64(x):
    return np.asarray(x).astype(np.float64)


EPS = 1e-5
NB, TS_D, SEG_NUM, D_MODEL, WIN = 4, 4, 511, 512, 2
K = WIN * D_MODEL
M1 = (SEG_NUM - 1) // WIN + 1


def merge(x, w):
    B, ts_d, seg_num, d = x.shape
    pad = (seg_num - 1) % w
    if pad != 0:
        pad = w - pad
        x = np.concatenate([x, x[:, :, -pad:, :]], axis=2)
    cls_tok = np.concatenate([x[:, :, :1, :]] * w, axis=-1)
    rest = x[:, :, 1:, :].reshape(B, ts_d, -1, w * d)
    return np.concatenate([cls_tok, rest], axis=2)


def setup_inputs():
    u = mx_kscale(D_MODEL)
    x = np.random.standard_normal((NB, TS_D, SEG_NUM, D_MODEL))
    gamma = 1.0 + 0.1 * np.random.standard_normal(K)
    beta = 0.1 * np.random.standard_normal(K)
    W = np.random.standard_normal((K, D_MODEL)) * 0.044 / u
    b = 0.1 * np.random.standard_normal(D_MODEL)
    g = (np.random.standard_normal((NB, TS_D, M1, D_MODEL))
         * np.exp2(np.random.randint(-12, 1, (NB, TS_D, M1, 1))) * 8.0 * u)
    return {"x": bf(x), "gamma": bf(gamma), "beta": bf(beta), "W": bf(W), "b": bf(b),
            "win_size": WIN, "grad_out": bf(g)}


def reference(x, gamma, beta, W, b, win_size, grad_out):
    x = f64(x)
    B, ts_d, seg_num, d = x.shape
    w = int(win_size)
    y = merge(x, w)
    mu = np.mean(y, axis=-1, keepdims=True)
    var = np.mean(np.square(y - mu), axis=-1, keepdims=True)
    r = 1.0 / np.sqrt(var + EPS)
    xh = (y - mu) * r
    dyn = mxq(f64(grad_out), 3, "e5m2") @ mxq(f64(W), 1, "e4m3").T
    dxh = dyn * f64(gamma)
    m1 = np.mean(dxh, axis=-1, keepdims=True)
    m2 = np.mean(dxh * xh, axis=-1, keepdims=True)
    dy = r * (dxh - m1 - xh * m2)
    d_cls = dy[:, :, :1, :].reshape(B, ts_d, w, d).sum(axis=2, keepdims=True)
    d_rest = dy[:, :, 1:, :].reshape(B, ts_d, -1, d)
    dxx = np.concatenate([d_cls, d_rest], axis=2)
    gx = dxx[:, :, :seg_num, :].copy()
    extra = dxx.shape[2] - seg_num
    if extra:
        gx[:, :, -extra:, :] += dxx[:, :, seg_num:, :]
    return gx

@@ -1,0 +1,199 @@
+from contextlib import ExitStack
+
+import concourse.mybir as mybir
+from concourse.masks import make_identity
+
+F32 = mybir.dt.float32
+BF16 = mybir.dt.bfloat16
+U32 = mybir.dt.uint32
+U8 = mybir.dt.uint8
+E4X4 = mybir.dt.float8_e4m3fn_x4
+E5X4 = mybir.dt.float8_e5m2_x4
+ALU = mybir.AluOpType
+ACT = mybir.ActivationFunctionType
+
+P = 128
+D = 512
+N = 1024
+SERIES = 16
+SEG = 511
+MROWS = 256
+EPS = 1e-5
+
+FLOPS = 2 * SERIES * MROWS * D * N
+
+
+def tile_segmerging_kernel(tc, x, gamma, beta, W, b, win_size, grad_out, out):
+    nc = tc.nc
+    x3 = x.rearrange("a b n d -> (a b) n d")
+    g3 = grad_out.rearrange("a b m d -> (a b) m d")
+    o3 = out.rearrange("a b n d -> (a b) n d")
+
+    with ExitStack() as ctx:
+        const = ctx.enter_context(tc.tile_pool(name="const", bufs=1))
+        ypool = ctx.enter_context(tc.tile_pool(name="ypool", bufs=12))
+        gpool = ctx.enter_context(tc.tile_pool(name="gpool", bufs=4))
+        qpool = ctx.enter_context(tc.tile_pool(name="qpool", bufs=3))
+        azpool = ctx.enter_context(tc.tile_pool(name="azpool", bufs=6))
+        tpool = ctx.enter_context(tc.tile_pool(name="tpool", bufs=4))
+        jpool = ctx.enter_context(tc.tile_pool(name="jpool", bufs=2))
+        small = ctx.enter_context(tc.tile_pool(name="small", bufs=8))
+        tp_ps = ctx.enter_context(tc.psum_pool(name="tp_ps", bufs=2))
+        dyn_ps = ctx.enter_context(tc.psum_pool(name="dyn_ps", bufs=3))
+
+        ident = const.tile([P, P], F32, name="ident")
+        make_identity(nc, ident[:])
+        eps_col = const.tile([P, 1], F32, name="eps_col")
+        nc.vector.memset(eps_col[:], EPS)
+
+        w_raw = const.tile([P, 8, D], BF16, name="w_raw")
+        for hf in range(2):
+            nc.sync.dma_start(
+                out=w_raw[:, 4 * hf:4 * hf + 4, :],
+                in_=W[512 * hf:512 * hf + 512, :].rearrange("(a p) k -> p a k", p=P),
+            )
+        gamma_bc = const.tile([P, N], BF16, name="gamma_bc")
+        nc.scalar.dma_start(out=gamma_bc[:], in_=gamma.partition_broadcast(P))
+
+        w_grp = const.tile([P, N, 4], BF16, name="w_grp", align_bytes=64)
+        w_grp32 = w_grp[:].bitcast(F32)
+        w_codes = const.tile([P, N], U32, name="w_codes", align_bytes=64)
+        w_scales = const.tile([P, N], U8, name="w_scales", align_bytes=64)
+        for q in range(4):
+            wt = tp_ps.tile([P, 2, 2, P], F32, name="wt", tag="tp")
+            for a2 in range(2):
+                src = w_raw[:, 2 * q + a2, :].bitcast(F32)
+                for u in range(2):
+                    nc.tensor.transpose(wt[:, a2, u, :], src[:, P * u:P * u + P], ident[:])
+            dst = w_grp32[:, 256 * q:256 * q + 256, :].rearrange("p (a j) u -> p a j u", a=2)
+            if q % 2 == 0:
+                nc.vector.tensor_copy(out=dst, in_=wt[:].rearrange("p a u j -> p a j u"))
+            else:
+                nc.scalar.copy(out=dst, in_=wt[:].rearrange("p a u j -> p a j u"))
+            if q % 2 == 1:
+                hf = q // 2
+                nc.vector.quantize_mx(
+                    out=w_codes[:, 512 * hf:512 * hf + 512].bitcast(E4X4),
+                    scales=w_scales[:, 512 * hf:512 * hf + 512],
+                    in_=w_grp[:, 512 * hf:512 * hf + 512, :].rearrange("p j t -> p (j t)"),
+                )
+
+        groups = [[("cls", 0, 0)]] + [[("reg", s, 0), ("reg", s, 1)] for s in range(SERIES)]
+
+        for grp in groups:
+            m = len(grp)
+            g_raw = gpool.tile([P, 2, D], BF16, name="g_raw")
+            ys = []
+            for h, (kind, s, hh) in enumerate(grp):
+                y = ypool.tile([P, N], BF16, name="y")
+                ys.append(y)
+                if kind == "cls":
+                    nc.vector.memset(g_raw[:, 0, :], 0.0)
+                    nc.vector.memset(y[:], 0.0)
+                    nc.sync.dma_start(out=g_raw[0:SERIES, 0, :], in_=g3[:, 0, :])
+                    nc.sync.dma_start(out=y[0:SERIES, 0:D], in_=x3[:, 0, :])
+                    nc.sync.dma_start(out=y[0:SERIES, D:N], in_=x3[:, 0, :])
+                else:
+                    m0 = 1 + 127 * hh
+                    r0 = 2 * m0 - 1
+                    nc.sync.dma_start(out=g_raw[:, h, :], in_=g3[s, m0:m0 + P, :])
+                    nc.sync.dma_start(
+                        out=y[:],
+                        in_=x3[s, r0:r0 + 2 * P, :].rearrange("(p r) c -> p (r c)", r=2),
+                    )
+
+            gt = tp_ps.tile([P, 2, 2, P], F32, name="gt", tag="tp")
+            for h in range(m):
+                src = g_raw[:, h, :].bitcast(F32)
+                for u in range(2):
+                    nc.tensor.transpose(gt[:, h, u, :], src[:, P * u:P * u + P], ident[:])
+            g_grp = qpool.tile([P, 2 * P, 4], BF16, name="g_grp", align_bytes=64)
+            g_codes = qpool.tile([P, 2 * P], U32, name="g_codes", align_bytes=64)
+            g_scales = qpool.tile([P, 2 * P], U8, name="g_scales", align_bytes=64)
+            nc.scalar.copy(
+                out=g_grp[:].bitcast(F32)[:, 0:P * m, :].rearrange("p (h t) u -> p h t u", h=m),
+                in_=gt[:, 0:m, :, :].rearrange("p h u t -> p h t u"),
+            )
+            nc.vector.quantize_mx(
+                out=g_codes[:, 0:P * m].bitcast(E5X4),
+                scales=g_scales[:, 0:P * m],
+                in_=g_grp[:, 0:P * m, :].rearrange("p t k -> p (t k)"),
+            )
+
+            sy = small.tile([P, 2], F32, name="sy")
+            negmu = small.tile([P, 2], F32, name="negmu")
+            ssq = small.tile([P, 2], F32, name="ssq")
+            sd = small.tile([P, 2], F32, name="sd")
+            rstd = small.tile([P, 2], F32, name="rstd")
+            r2 = small.tile([P, 2], F32, name="r2")
+            nr2n = small.tile([P, 2], F32, name="nr2n")
+            k2 = small.tile([P, 2], F32, name="k2")
+            for h in range(m):
+                junk = jpool.tile([P, N], BF16, name="junk")
+                nc.scalar.activation(out=junk[:], in_=ys[h][:], func=ACT.Identity,
+                                     accum_out=sy[:, h:h + 1])
+            nc.scalar.mul(out=negmu[:, 0:m], in_=sy[:, 0:m], mul=-1.0 / N)
+            for h in range(m):
+                junk = jpool.tile([P, N], BF16, name="junk")
+                nc.scalar.activation(out=junk[:], in_=ys[h][:], func=ACT.Square,
+                                     bias=negmu[:, h:h + 1], scale=1.0,
+                                     accum_out=ssq[:, h:h + 1])
+            nc.scalar.activation(out=sd[:, 0:m], in_=ssq[:, 0:m], func=ACT.Sqrt,
+                                 bias=eps_col[:], scale=1.0 / N)
+            nc.vector.reciprocal(out=rstd[:, 0:m], in_=sd[:, 0:m])
+            nc.gpsimd.tensor_tensor(out=r2[:, 0:m], in0=rstd[:, 0:m], in1=rstd[:, 0:m], op=ALU.mult)
+            nc.gpsimd.tensor_scalar(out=nr2n[:, 0:m], in0=r2[:, 0:m], scalar1=-1.0 / N, scalar2=0.0,
+                                    op0=ALU.mult, op1=ALU.add)
+            nc.gpsimd.tensor_tensor(out=k2[:, 0:m], in0=nr2n[:, 0:m], in1=negmu[:, 0:m], op=ALU.mult)
+
+            for h, (kind, s, hh) in enumerate(grp):
+                y = ys[h]
+                dyn = []
+                for hf in range(2):
+                    acc = dyn_ps.tile([P, 512], F32, name="acc%d" % hf)
+                    nc.tensor.matmul_mx(
+                        out=acc[:],
+                        lhsT=g_codes[:, P * h:P * h + P].bitcast(E5X4),
+                        lhsT_scale=g_scales[:, P * h:P * h + P],
+                        rhs=w_codes[:, 512 * hf:512 * hf + 512].bitcast(E4X4),
+                        rhs_scale=w_scales[:, 512 * hf:512 * hf + 512],
+                        start=True,
+                        stop=True,
+                    )
+                    dyn.append(acc)
+                az = azpool.tile([P, N], F32, name="az")
+                s1 = small.tile([P, 2], F32, name="s1")
+                for hf in range(2):
+                    nc.vector.scalar_tensor_tensor(
+                        out=az[:, 512 * hf:512 * hf + 512], in0=dyn[hf][:],
+                        scalar=rstd[:, h:h + 1], in1=gamma_bc[:, 512 * hf:512 * hf + 512],
+                        op0=ALU.mult, op1=ALU.mult, accum_out=s1[:, hf:hf + 1],
+                    )
+                t = tpool.tile([P, N], F32, name="t")
+                dot = small.tile([P, 1], F32, name="dot")
+                nc.vector.scalar_tensor_tensor(
+                    out=t[:], in0=y[:], scalar=negmu[:, h:h + 1], in1=az[:],
+                    op0=ALU.add, op1=ALU.mult, accum_out=dot[:],
+                )
+                e1 = small.tile([P, 1], F32, name="e1")
+                bcol = small.tile([P, 1], F32, name="bcol")
+                ccol = small.tile([P, 1], F32, name="ccol")
+                nc.gpsimd.tensor_scalar(out=e1[:], in0=s1[:, 0:1], scalar1=s1[:, 1:2],
+                                        scalar2=-1.0 / N, op0=ALU.add, op1=ALU.mult)
+                nc.gpsimd.tensor_tensor(out=bcol[:], in0=dot[:], in1=nr2n[:, h:h + 1], op=ALU.mult)
+                nc.gpsimd.tensor_scalar(out=ccol[:], in0=dot[:], scalar1=k2[:, h:h + 1],
+                                        scalar2=e1[:], op0=ALU.mult, op1=ALU.add)
+                nc.scalar.activation(out=t[:], in_=y[:], func=ACT.Identity,
+                                     scale=bcol[:], bias=ccol[:])
+                nc.vector.tensor_tensor(out=az[:], in0=az[:], in1=t[:], op=ALU.add)
+                if kind == "cls":
+                    cls = const.tile([P, D], F32, name="cls")
+                    nc.vector.tensor_tensor(out=cls[0:32, :], in0=az[0:32, 0:D], in1=az[0:32, D:N],
+                                            op=ALU.add)
+                    nc.sync.dma_start(out=o3[:, 0, :], in_=cls[0:SERIES, :])
+                else:
+                    r0 = 2 * (1 + 127 * hh) - 1
+                    nc.sync.dma_start(
+                        out=o3[s, r0:r0 + 2 * P, :].rearrange("(p r) c -> p (r c)", r=2),
+                        in_=az[:],
+                    )

@@ -16,11 +16,13 @@ P = 128
 D = 512
 N = 1024
 SERIES = 16
-SEG = 511
-MROWS = 256
 EPS = 1e-5
+MROWS = 256
 
 FLOPS = 2 * SERIES * MROWS * D * N
+
+LAG = 3
+TAIL_S = 3
 
 
 def tile_segmerging_kernel(tc, x, gamma, beta, W, b, win_size, grad_out, out):
@@ -29,171 +31,327 @@ def tile_segmerging_kernel(tc, x, gamma, beta, W, b, win_size, grad_out, out):
     g3 = grad_out.rearrange("a b m d -> (a b) m d")
     o3 = out.rearrange("a b n d -> (a b) n d")
 
+    groups = [[0]] + [[2 * k - 1, 2 * k] for k in range(1, SERIES + 1)]
+    NG = len(groups)
+    NT = 2 * SERIES + 1
+
+    def grp_of(n):
+        return (n + 1) // 2
+
+    def idx_in_grp(n):
+        return 0 if n == 0 else (n - 1) % 2
+
     with ExitStack() as ctx:
         const = ctx.enter_context(tc.tile_pool(name="const", bufs=1))
-        ypool = ctx.enter_context(tc.tile_pool(name="ypool", bufs=12))
+        ypool = ctx.enter_context(tc.tile_pool(name="ypool", bufs=14))
         gpool = ctx.enter_context(tc.tile_pool(name="gpool", bufs=4))
         qpool = ctx.enter_context(tc.tile_pool(name="qpool", bufs=3))
-        azpool = ctx.enter_context(tc.tile_pool(name="azpool", bufs=6))
-        tpool = ctx.enter_context(tc.tile_pool(name="tpool", bufs=4))
+        azpool = ctx.enter_context(tc.tile_pool(name="azpool", bufs=7))
+        tpool = ctx.enter_context(tc.tile_pool(name="tpool", bufs=5))
         jpool = ctx.enter_context(tc.tile_pool(name="jpool", bufs=2))
         small = ctx.enter_context(tc.tile_pool(name="small", bufs=8))
         tp_ps = ctx.enter_context(tc.psum_pool(name="tp_ps", bufs=2))
         dyn_ps = ctx.enter_context(tc.psum_pool(name="dyn_ps", bufs=3))
+        ctx.enter_context(tc.manual_schedule())
+
+        g_raw = {}
+        ys = {}
+        gts = {}
+        g_grp = {}
+        g_q = {}
+        st = {}
+        acc = {}
+        azs = {}
+        ts = {}
+        per = {}
 
         ident = const.tile([P, P], F32, name="ident")
         make_identity(nc, ident[:])
         eps_col = const.tile([P, 1], F32, name="eps_col")
         nc.vector.memset(eps_col[:], EPS)
+        warm = const.tile([P, 1], F32, name="warm")
+        nc.scalar.activation(out=warm[:], in_=eps_col[:], func=ACT.Sqrt)
 
         w_raw = const.tile([P, 8, D], BF16, name="w_raw")
-        for hf in range(2):
-            nc.sync.dma_start(
-                out=w_raw[:, 4 * hf:4 * hf + 4, :],
-                in_=W[512 * hf:512 * hf + 512, :].rearrange("(a p) k -> p a k", p=P),
-            )
+        gamma_row = const.tile([P, N], BF16, name="gamma_row")
+        ones = const.tile([P, P], BF16, name="ones")
         gamma_bc = const.tile([P, N], BF16, name="gamma_bc")
-        nc.scalar.dma_start(out=gamma_bc[:], in_=gamma.partition_broadcast(P))
-
         w_grp = const.tile([P, N, 4], BF16, name="w_grp", align_bytes=64)
         w_grp32 = w_grp[:].bitcast(F32)
         w_codes = const.tile([P, N], U32, name="w_codes", align_bytes=64)
         w_scales = const.tile([P, N], U8, name="w_scales", align_bytes=64)
-        for q in range(4):
+        cls = const.tile([P, D], F32, name="cls")
+
+        def load_w(hf):
+            nc.sync.dma_start(
+                out=w_raw[:, 4 * hf:4 * hf + 4, :],
+                in_=W[512 * hf:512 * hf + 512, :].rearrange("(a p) k -> p a k", p=P),
+            )
+
+        def load(k):
+            if k >= NG:
+                return
+            gr = gpool.tile([P, 2, D], BF16, name="g_raw")
+            g_raw[k] = gr
+            for h, n in enumerate(groups[k]):
+                y = ypool.tile([P, N], BF16, name="y")
+                ys[n] = y
+                if n == 0:
+                    nc.vector.memset(gr[:, 0, :], 0.0)
+                    nc.vector.memset(y[:], 0.0)
+                    nc.sync.dma_start(out=gr[0:SERIES, 0, :], in_=g3[:, 0, :])
+                    nc.sync.dma_start(out=y[0:SERIES, 0:D], in_=x3[:, 0, :])
+                    nc.sync.dma_start(out=y[0:SERIES, D:N], in_=x3[:, 0, :])
+                else:
+                    m0 = 1 + 127 * h
+                    r0 = 2 * m0 - 1
+                    nc.sync.dma_start(out=gr[:, h, :], in_=g3[k - 1, m0:m0 + P, :])
+                    nc.sync.dma_start(
+                        out=y[:],
+                        in_=x3[k - 1, r0:r0 + 2 * P, :].rearrange("(p r) c -> p (r c)", r=2),
+                    )
+
+        def w_transpose(q):
             wt = tp_ps.tile([P, 2, 2, P], F32, name="wt", tag="tp")
             for a2 in range(2):
                 src = w_raw[:, 2 * q + a2, :].bitcast(F32)
                 for u in range(2):
                     nc.tensor.transpose(wt[:, a2, u, :], src[:, P * u:P * u + P], ident[:])
+            return wt
+
+        def w_copy(q, wt, eng):
             dst = w_grp32[:, 256 * q:256 * q + 256, :].rearrange("p (a j) u -> p a j u", a=2)
-            if q % 2 == 0:
+            if eng == "v":
                 nc.vector.tensor_copy(out=dst, in_=wt[:].rearrange("p a u j -> p a j u"))
             else:
                 nc.scalar.copy(out=dst, in_=wt[:].rearrange("p a u j -> p a j u"))
-            if q % 2 == 1:
-                hf = q // 2
-                nc.vector.quantize_mx(
-                    out=w_codes[:, 512 * hf:512 * hf + 512].bitcast(E4X4),
-                    scales=w_scales[:, 512 * hf:512 * hf + 512],
-                    in_=w_grp[:, 512 * hf:512 * hf + 512, :].rearrange("p j t -> p (j t)"),
-                )
 
-        groups = [[("cls", 0, 0)]] + [[("reg", s, 0), ("reg", s, 1)] for s in range(SERIES)]
+        def w_quant(hf):
+            nc.vector.quantize_mx(
+                out=w_codes[:, 512 * hf:512 * hf + 512].bitcast(E4X4),
+                scales=w_scales[:, 512 * hf:512 * hf + 512],
+                in_=w_grp[:, 512 * hf:512 * hf + 512, :].rearrange("p j t -> p (j t)"),
+            )
 
-        for grp in groups:
-            m = len(grp)
-            g_raw = gpool.tile([P, 2, D], BF16, name="g_raw")
-            ys = []
-            for h, (kind, s, hh) in enumerate(grp):
-                y = ypool.tile([P, N], BF16, name="y")
-                ys.append(y)
-                if kind == "cls":
-                    nc.vector.memset(g_raw[:, 0, :], 0.0)
-                    nc.vector.memset(y[:], 0.0)
-                    nc.sync.dma_start(out=g_raw[0:SERIES, 0, :], in_=g3[:, 0, :])
-                    nc.sync.dma_start(out=y[0:SERIES, 0:D], in_=x3[:, 0, :])
-                    nc.sync.dma_start(out=y[0:SERIES, D:N], in_=x3[:, 0, :])
-                else:
-                    m0 = 1 + 127 * hh
-                    r0 = 2 * m0 - 1
-                    nc.sync.dma_start(out=g_raw[:, h, :], in_=g3[s, m0:m0 + P, :])
-                    nc.sync.dma_start(
-                        out=y[:],
-                        in_=x3[s, r0:r0 + 2 * P, :].rearrange("(p r) c -> p (r c)", r=2),
-                    )
-
+        def g_transpose(k):
+            if k >= NG:
+                return
             gt = tp_ps.tile([P, 2, 2, P], F32, name="gt", tag="tp")
-            for h in range(m):
-                src = g_raw[:, h, :].bitcast(F32)
+            gts[k] = gt
+            for h in range(len(groups[k])):
+                src = g_raw[k][:, h, :].bitcast(F32)
                 for u in range(2):
                     nc.tensor.transpose(gt[:, h, u, :], src[:, P * u:P * u + P], ident[:])
-            g_grp = qpool.tile([P, 2 * P, 4], BF16, name="g_grp", align_bytes=64)
-            g_codes = qpool.tile([P, 2 * P], U32, name="g_codes", align_bytes=64)
-            g_scales = qpool.tile([P, 2 * P], U8, name="g_scales", align_bytes=64)
-            nc.scalar.copy(
-                out=g_grp[:].bitcast(F32)[:, 0:P * m, :].rearrange("p (h t) u -> p h t u", h=m),
-                in_=gt[:, 0:m, :, :].rearrange("p h u t -> p h t u"),
-            )
+
+        def g_copy(k, eng):
+            if k >= NG:
+                return
+            m = len(groups[k])
+            gg = qpool.tile([P, 2 * P, 4], BF16, name="g_grp", align_bytes=64)
+            g_grp[k] = gg
+            dst = gg[:].bitcast(F32)[:, 0:P * m, :].rearrange("p (h t) u -> p h t u", h=m)
+            src = gts[k][:, 0:m, :, :].rearrange("p h u t -> p h t u")
+            if eng == "v":
+                nc.vector.tensor_copy(out=dst, in_=src)
+            else:
+                nc.scalar.copy(out=dst, in_=src)
+
+        def g_quant(k):
+            if k >= NG:
+                return
+            m = len(groups[k])
+            codes = qpool.tile([P, 2 * P], U32, name="g_codes", align_bytes=64)
+            scales = qpool.tile([P, 2 * P], U8, name="g_scales", align_bytes=64)
+            g_q[k] = (codes, scales)
             nc.vector.quantize_mx(
-                out=g_codes[:, 0:P * m].bitcast(E5X4),
-                scales=g_scales[:, 0:P * m],
-                in_=g_grp[:, 0:P * m, :].rearrange("p t k -> p (t k)"),
+                out=codes[:, 0:P * m].bitcast(E5X4),
+                scales=scales[:, 0:P * m],
+                in_=g_grp[k][:, 0:P * m, :].rearrange("p t k -> p (t k)"),
             )
 
-            sy = small.tile([P, 2], F32, name="sy")
-            negmu = small.tile([P, 2], F32, name="negmu")
-            ssq = small.tile([P, 2], F32, name="ssq")
-            sd = small.tile([P, 2], F32, name="sd")
-            rstd = small.tile([P, 2], F32, name="rstd")
-            r2 = small.tile([P, 2], F32, name="r2")
-            nr2n = small.tile([P, 2], F32, name="nr2n")
-            k2 = small.tile([P, 2], F32, name="k2")
-            for h in range(m):
+        def stat_unit(k, r):
+            if k >= NG:
+                return
+            m = len(groups[k])
+            if r == 0:
+                st[k] = {}
+                for nm in ("sy", "negmu", "ssq", "sd", "rstd", "r2n"):
+                    st[k][nm] = small.tile([P, 2], F32, name=nm)
+            s = st[k]
+            h = r % 2
+            if h < m:
                 junk = jpool.tile([P, N], BF16, name="junk")
-                nc.scalar.activation(out=junk[:], in_=ys[h][:], func=ACT.Identity,
-                                     accum_out=sy[:, h:h + 1])
-            nc.scalar.mul(out=negmu[:, 0:m], in_=sy[:, 0:m], mul=-1.0 / N)
-            for h in range(m):
-                junk = jpool.tile([P, N], BF16, name="junk")
-                nc.scalar.activation(out=junk[:], in_=ys[h][:], func=ACT.Square,
-                                     bias=negmu[:, h:h + 1], scale=1.0,
-                                     accum_out=ssq[:, h:h + 1])
-            nc.scalar.activation(out=sd[:, 0:m], in_=ssq[:, 0:m], func=ACT.Sqrt,
-                                 bias=eps_col[:], scale=1.0 / N)
-            nc.vector.reciprocal(out=rstd[:, 0:m], in_=sd[:, 0:m])
-            nc.gpsimd.tensor_tensor(out=r2[:, 0:m], in0=rstd[:, 0:m], in1=rstd[:, 0:m], op=ALU.mult)
-            nc.gpsimd.tensor_scalar(out=nr2n[:, 0:m], in0=r2[:, 0:m], scalar1=-1.0 / N, scalar2=0.0,
-                                    op0=ALU.mult, op1=ALU.add)
-            nc.gpsimd.tensor_tensor(out=k2[:, 0:m], in0=nr2n[:, 0:m], in1=negmu[:, 0:m], op=ALU.mult)
-
-            for h, (kind, s, hh) in enumerate(grp):
-                y = ys[h]
-                dyn = []
-                for hf in range(2):
-                    acc = dyn_ps.tile([P, 512], F32, name="acc%d" % hf)
-                    nc.tensor.matmul_mx(
-                        out=acc[:],
-                        lhsT=g_codes[:, P * h:P * h + P].bitcast(E5X4),
-                        lhsT_scale=g_scales[:, P * h:P * h + P],
-                        rhs=w_codes[:, 512 * hf:512 * hf + 512].bitcast(E4X4),
-                        rhs_scale=w_scales[:, 512 * hf:512 * hf + 512],
-                        start=True,
-                        stop=True,
-                    )
-                    dyn.append(acc)
-                az = azpool.tile([P, N], F32, name="az")
-                s1 = small.tile([P, 2], F32, name="s1")
-                for hf in range(2):
-                    nc.vector.scalar_tensor_tensor(
-                        out=az[:, 512 * hf:512 * hf + 512], in0=dyn[hf][:],
-                        scalar=rstd[:, h:h + 1], in1=gamma_bc[:, 512 * hf:512 * hf + 512],
-                        op0=ALU.mult, op1=ALU.mult, accum_out=s1[:, hf:hf + 1],
-                    )
-                t = tpool.tile([P, N], F32, name="t")
-                dot = small.tile([P, 1], F32, name="dot")
-                nc.vector.scalar_tensor_tensor(
-                    out=t[:], in0=y[:], scalar=negmu[:, h:h + 1], in1=az[:],
-                    op0=ALU.add, op1=ALU.mult, accum_out=dot[:],
-                )
-                e1 = small.tile([P, 1], F32, name="e1")
-                bcol = small.tile([P, 1], F32, name="bcol")
-                ccol = small.tile([P, 1], F32, name="ccol")
-                nc.gpsimd.tensor_scalar(out=e1[:], in0=s1[:, 0:1], scalar1=s1[:, 1:2],
-                                        scalar2=-1.0 / N, op0=ALU.add, op1=ALU.mult)
-                nc.gpsimd.tensor_tensor(out=bcol[:], in0=dot[:], in1=nr2n[:, h:h + 1], op=ALU.mult)
-                nc.gpsimd.tensor_scalar(out=ccol[:], in0=dot[:], scalar1=k2[:, h:h + 1],
-                                        scalar2=e1[:], op0=ALU.mult, op1=ALU.add)
-                nc.scalar.activation(out=t[:], in_=y[:], func=ACT.Identity,
-                                     scale=bcol[:], bias=ccol[:])
-                nc.vector.tensor_tensor(out=az[:], in0=az[:], in1=t[:], op=ALU.add)
-                if kind == "cls":
-                    cls = const.tile([P, D], F32, name="cls")
-                    nc.vector.tensor_tensor(out=cls[0:32, :], in0=az[0:32, 0:D], in1=az[0:32, D:N],
-                                            op=ALU.add)
-                    nc.sync.dma_start(out=o3[:, 0, :], in_=cls[0:SERIES, :])
+                y = ys[groups[k][h]]
+                if r < 2:
+                    nc.scalar.activation(out=junk[:], in_=y[:], func=ACT.Identity,
+                                         accum_out=s["sy"][:, h:h + 1])
                 else:
-                    r0 = 2 * (1 + 127 * hh) - 1
-                    nc.sync.dma_start(
-                        out=o3[s, r0:r0 + 2 * P, :].rearrange("(p r) c -> p (r c)", r=2),
-                        in_=az[:],
-                    )
+                    nc.scalar.activation(out=junk[:], in_=y[:], func=ACT.Square,
+                                         bias=s["negmu"][:, h:h + 1], scale=1.0,
+                                         accum_out=s["ssq"][:, h:h + 1])
+            if r == 1:
+                nc.scalar.mul(out=s["negmu"][:, 0:m], in_=s["sy"][:, 0:m], mul=-1.0 / N)
+            if r == 3:
+                nc.scalar.activation(out=s["sd"][:, 0:m], in_=s["ssq"][:, 0:m], func=ACT.Sqrt,
+                                     bias=eps_col[:], scale=1.0 / N)
+
+        def stat_finish(k):
+            if k >= NG:
+                return
+            m = len(groups[k])
+            s = st[k]
+            nc.vector.reciprocal(out=s["rstd"][:, 0:m], in_=s["sd"][:, 0:m])
+            nc.scalar.activation(out=s["r2n"][:, 0:m], in_=s["rstd"][:, 0:m], func=ACT.Square,
+                                 scale=1.0 / 32.0)
+
+        def mx_half(n, hf):
+            k = grp_of(n)
+            h = idx_in_grp(n)
+            codes, scales = g_q[k]
+            a = dyn_ps.tile([P, 512], F32, name="acc%d" % hf)
+            nc.tensor.matmul_mx(
+                out=a[:],
+                lhsT=codes[:, P * h:P * h + P].bitcast(E5X4),
+                lhsT_scale=scales[:, P * h:P * h + P],
+                rhs=w_codes[:, 512 * hf:512 * hf + 512].bitcast(E4X4),
+                rhs_scale=w_scales[:, 512 * hf:512 * hf + 512],
+                start=True, stop=True,
+            )
+            acc[(n, hf)] = a
+
+        def mx(n):
+            if n >= NT:
+                return
+            mx_half(n, 0)
+            mx_half(n, 1)
+
+        def a_half(n, hf):
+            s = st[grp_of(n)]
+            h = idx_in_grp(n)
+            if hf == 0:
+                azs[n] = azpool.tile([P, N], F32, name="az")
+                per[n] = {}
+                for nm, w in (("s1", 2), ("dot", 1), ("s1j", 2), ("ne1", 1), ("nb", 1), ("nc", 1)):
+                    per[n][nm] = small.tile([P, w], F32, name=nm)
+            nc.vector.scalar_tensor_tensor(
+                out=azs[n][:, 512 * hf:512 * hf + 512], in0=acc[(n, hf)][:],
+                scalar=s["rstd"][:, h:h + 1], in1=gamma_bc[:, 512 * hf:512 * hf + 512],
+                op0=ALU.mult, op1=ALU.mult, accum_out=per[n]["s1"][:, hf:hf + 1],
+            )
+
+        def pass_b(n):
+            s = st[grp_of(n)]
+            h = idx_in_grp(n)
+            t = tpool.tile([P, N], F32, name="t")
+            ts[n] = t
+            nc.vector.scalar_tensor_tensor(
+                out=t[:], in0=ys[n][:], scalar=s["negmu"][:, h:h + 1], in1=azs[n][:],
+                op0=ALU.add, op1=ALU.mult, accum_out=per[n]["dot"][:],
+            )
+
+        def coeffs(n):
+            if n < 0 or n >= NT:
+                return
+            s = st[grp_of(n)]
+            h = idx_in_grp(n)
+            p = per[n]
+            nc.scalar.activation(out=p["s1j"][:], in_=p["s1"][:], func=ACT.Copy, scale=1.0 / N,
+                                 accum_out=p["ne1"][:])
+            nc.scalar.activation(out=p["nb"][:], in_=p["dot"][:], func=ACT.Copy,
+                                 scale=s["r2n"][:, h:h + 1])
+            nc.scalar.activation(out=p["nc"][:], in_=p["nb"][:], func=ACT.Identity,
+                                 scale=s["negmu"][:, h:h + 1], bias=p["ne1"][:])
+
+        def pass_t(n, eng):
+            if n < 0 or n >= NT:
+                return
+            p = per[n]
+            if eng == "s":
+                nc.scalar.activation(out=ts[n][:], in_=ys[n][:], func=ACT.Identity,
+                                     scale=p["nb"][:], bias=p["nc"][:])
+            else:
+                nc.gpsimd.tensor_scalar(out=ts[n][:], in0=ys[n][:], scalar1=p["nb"][:],
+                                        scalar2=p["nc"][:], op0=ALU.mult, op1=ALU.add)
+
+        def pass_e(n):
+            if n < 0 or n >= NT:
+                return
+            az = azs[n]
+            nc.vector.tensor_tensor(out=az[:], in0=az[:], in1=ts[n][:], op=ALU.subtract)
+            if n == 0:
+                nc.vector.tensor_tensor(out=cls[0:32, :], in0=az[0:32, 0:D], in1=az[0:32, D:N],
+                                        op=ALU.add)
+                nc.sync.dma_start(out=o3[:, 0, :], in_=cls[0:SERIES, :])
+            else:
+                r0 = 2 * (1 + 127 * idx_in_grp(n)) - 1
+                nc.sync.dma_start(
+                    out=o3[grp_of(n) - 1, r0:r0 + 2 * P, :].rearrange("(p r) c -> p (r c)", r=2),
+                    in_=az[:],
+                )
+
+        nc.vector.memset(gamma_row[:], 0.0)
+        nc.vector.memset(ones[:], 1.0)
+        nc.scalar.dma_start(out=gamma_row[0:1, :], in_=gamma.unsqueeze(0))
+        load_w(0)
+        load(0)
+        load_w(1)
+        for k in range(1, 5):
+            load(k)
+        for hf in range(2):
+            gp = dyn_ps.tile([P, 512], F32, name="acc%d" % hf)
+            nc.tensor.matmul(out=gp[:], lhsT=ones[:], rhs=gamma_row[:, 512 * hf:512 * hf + 512],
+                             start=True, stop=True)
+            nc.scalar.copy(out=gamma_bc[:, 512 * hf:512 * hf + 512], in_=gp[:])
+        g_transpose(0)
+        g_copy(0, "v")
+        g_quant(0)
+        stat_unit(0, 0)
+        stat_unit(0, 1)
+        wt0 = w_transpose(0)
+        w_copy(0, wt0, "v")
+        wt1 = w_transpose(1)
+        w_copy(1, wt1, "s")
+        w_quant(0)
+        stat_unit(0, 2)
+        stat_unit(0, 3)
+        wt2 = w_transpose(2)
+        w_copy(2, wt2, "v")
+        wt3 = w_transpose(3)
+        w_copy(3, wt3, "s")
+        stat_finish(0)
+        mx_half(0, 0)
+        a_half(0, 0)
+        w_quant(1)
+        mx_half(0, 1)
+        a_half(0, 1)
+        g_transpose(1)
+        g_copy(1, "s")
+        g_quant(1)
+        mx(1)
+        g_transpose(2)
+        for r in range(4):
+            stat_unit(1, r)
+
+        for n in range(NT + LAG):
+            if n % 2 == 1:
+                load((n + 9) // 2)
+                g_transpose((n + 5) // 2)
+                g_quant((n + 3) // 2)
+                stat_finish((n + 1) // 2)
+            else:
+                g_copy((n + 4) // 2, "s")
+            mx(n + 2)
+            k_stat = 2 + n // 2
+            stat_unit(k_stat, 2 * (n % 2))
+            if 0 < n < NT:
+                a_half(n, 0)
+                a_half(n, 1)
+            coeffs(n - 1)
+            if n - 1 >= NT - TAIL_S:
+                pass_t(n - 1, "s")
+            if n - 2 < NT - TAIL_S:
+                pass_t(n - 2, "g")
+            pass_e(n - LAG)
+            if n < NT:
+                pass_b(n)
+            stat_unit(k_stat, 2 * (n % 2) + 1)

@@ -21,8 +21,7 @@ MROWS = 256
 
 FLOPS = 2 * SERIES * MROWS * D * N
 
-LAG = 3
-TAIL_S = 3
+LAG = 2
 
 
 def tile_segmerging_kernel(tc, x, gamma, beta, W, b, win_size, grad_out, out):
@@ -189,20 +188,37 @@ def tile_segmerging_kernel(tc, x, gamma, beta, W, b, win_size, grad_out, out):
                     nc.scalar.activation(out=junk[:], in_=y[:], func=ACT.Square,
                                          bias=s["negmu"][:, h:h + 1], scale=1.0,
                                          accum_out=s["ssq"][:, h:h + 1])
-            if r == 1:
-                nc.scalar.mul(out=s["negmu"][:, 0:m], in_=s["sy"][:, 0:m], mul=-1.0 / N)
-            if r == 3:
-                nc.scalar.activation(out=s["sd"][:, 0:m], in_=s["ssq"][:, 0:m], func=ACT.Sqrt,
-                                     bias=eps_col[:], scale=1.0 / N)
 
-        def stat_finish(k):
+        def stat_negmu(k):
+            if k >= NG:
+                return
+            m = len(groups[k])
+            s = st[k]
+            nc.scalar.mul(out=s["negmu"][:, 0:m], in_=s["sy"][:, 0:m], mul=-1.0 / N)
+
+        def stat_sqrt(k):
+            if k >= NG:
+                return
+            m = len(groups[k])
+            s = st[k]
+            nc.scalar.activation(out=s["sd"][:, 0:m], in_=s["ssq"][:, 0:m], func=ACT.Sqrt,
+                                 bias=eps_col[:], scale=1.0 / N)
+
+        def stat_recip(k):
             if k >= NG:
                 return
             m = len(groups[k])
             s = st[k]
             nc.vector.reciprocal(out=s["rstd"][:, 0:m], in_=s["sd"][:, 0:m])
-            nc.scalar.activation(out=s["r2n"][:, 0:m], in_=s["rstd"][:, 0:m], func=ACT.Square,
-                                 scale=1.0 / 32.0)
+
+        def stat_r2n(k):
+            if k >= NG:
+                return
+            m = len(groups[k])
+            s = st[k]
+            nc.vector.scalar_tensor_tensor(
+                out=s["r2n"][:, 0:m], in0=s["rstd"][:, 0:m], scalar=1.0 / N,
+                in1=s["rstd"][:, 0:m], op0=ALU.mult, op1=ALU.mult)
 
         def mx_half(n, hf):
             k = grp_of(n)
@@ -231,7 +247,7 @@ def tile_segmerging_kernel(tc, x, gamma, beta, W, b, win_size, grad_out, out):
             if hf == 0:
                 azs[n] = azpool.tile([P, N], F32, name="az")
                 per[n] = {}
-                for nm, w in (("s1", 2), ("dot", 1), ("s1j", 2), ("ne1", 1), ("nb", 1), ("nc", 1)):
+                for nm, w in (("s1", 2), ("dot", 1), ("ne1", 1), ("nb", 1), ("nc", 1)):
                     per[n][nm] = small.tile([P, w], F32, name=nm)
             nc.vector.scalar_tensor_tensor(
                 out=azs[n][:, 512 * hf:512 * hf + 512], in0=acc[(n, hf)][:],
@@ -249,18 +265,30 @@ def tile_segmerging_kernel(tc, x, gamma, beta, W, b, win_size, grad_out, out):
                 op0=ALU.add, op1=ALU.mult, accum_out=per[n]["dot"][:],
             )
 
-        def coeffs(n):
+        def coef_ne1(n):
+            if n < 0 or n >= NT:
+                return
+            p = per[n]
+            nc.vector.tensor_scalar(out=p["ne1"][:], in0=p["s1"][:, 0:1], scalar1=p["s1"][:, 1:2],
+                                    scalar2=1.0 / N, op0=ALU.add, op1=ALU.mult)
+
+        def coef_nb(n):
             if n < 0 or n >= NT:
                 return
             s = st[grp_of(n)]
             h = idx_in_grp(n)
             p = per[n]
-            nc.scalar.activation(out=p["s1j"][:], in_=p["s1"][:], func=ACT.Copy, scale=1.0 / N,
-                                 accum_out=p["ne1"][:])
-            nc.scalar.activation(out=p["nb"][:], in_=p["dot"][:], func=ACT.Copy,
-                                 scale=s["r2n"][:, h:h + 1])
-            nc.scalar.activation(out=p["nc"][:], in_=p["nb"][:], func=ACT.Identity,
-                                 scale=s["negmu"][:, h:h + 1], bias=p["ne1"][:])
+            nc.vector.tensor_scalar(out=p["nb"][:], in0=p["dot"][:], scalar1=s["r2n"][:, h:h + 1],
+                                    scalar2=None, op0=ALU.mult)
+
+        def coef_nc(n):
+            if n < 0 or n >= NT:
+                return
+            s = st[grp_of(n)]
+            h = idx_in_grp(n)
+            p = per[n]
+            nc.vector.tensor_scalar(out=p["nc"][:], in0=p["nb"][:], scalar1=s["negmu"][:, h:h + 1],
+                                    scalar2=p["ne1"][:], op0=ALU.mult, op1=ALU.add)
 
         def pass_t(n, eng):
             if n < 0 or n >= NT:
@@ -306,52 +334,70 @@ def tile_segmerging_kernel(tc, x, gamma, beta, W, b, win_size, grad_out, out):
         g_copy(0, "v")
         g_quant(0)
         stat_unit(0, 0)
-        stat_unit(0, 1)
         wt0 = w_transpose(0)
         w_copy(0, wt0, "v")
         wt1 = w_transpose(1)
         w_copy(1, wt1, "s")
+        stat_negmu(0)
         w_quant(0)
         stat_unit(0, 2)
-        stat_unit(0, 3)
         wt2 = w_transpose(2)
         w_copy(2, wt2, "v")
         wt3 = w_transpose(3)
         w_copy(3, wt3, "s")
-        stat_finish(0)
+        stat_sqrt(0)
+        stat_recip(0)
         mx_half(0, 0)
-        a_half(0, 0)
         w_quant(1)
+        stat_r2n(0)
+        a_half(0, 0)
         mx_half(0, 1)
         a_half(0, 1)
         g_transpose(1)
+        stat_unit(1, 0)
+        stat_unit(1, 1)
         g_copy(1, "s")
+        stat_negmu(1)
         g_quant(1)
         mx(1)
         g_transpose(2)
-        for r in range(4):
-            stat_unit(1, r)
+        stat_unit(1, 2)
+        stat_unit(1, 3)
 
         for n in range(NT + LAG):
-            if n % 2 == 1:
+            odd = n % 2 == 1
+            k_stat = 2 + n // 2
+            k_next = (n + 2) // 2
+            if odd:
                 load((n + 9) // 2)
                 g_transpose((n + 5) // 2)
-                g_quant((n + 3) // 2)
-                stat_finish((n + 1) // 2)
-            else:
-                g_copy((n + 4) // 2, "s")
             mx(n + 2)
-            k_stat = 2 + n // 2
-            stat_unit(k_stat, 2 * (n % 2))
+            if odd:
+                stat_negmu(k_stat)
+                stat_unit(k_stat, 2)
+                stat_unit(k_stat, 3)
+            else:
+                if n == 0:
+                    stat_sqrt(1)
+                g_copy((n + 4) // 2, "s")
+                stat_unit(k_stat, 0)
+                stat_unit(k_stat, 1)
             if 0 < n < NT:
                 a_half(n, 0)
+            coef_nb(n - 1)
+            if 0 < n < NT:
                 a_half(n, 1)
-            coeffs(n - 1)
-            if n - 1 >= NT - TAIL_S:
-                pass_t(n - 1, "s")
-            if n - 2 < NT - TAIL_S:
-                pass_t(n - 2, "g")
+            coef_nc(n - 1)
+            pass_t(n - 1, "s")
+            if odd:
+                stat_sqrt(k_stat)
             pass_e(n - LAG)
             if n < NT:
+                coef_ne1(n)
+            if odd:
+                stat_r2n((n + 1) // 2)
+            if n < NT:
                 pass_b(n)
-            stat_unit(k_stat, 2 * (n % 2) + 1)
+            if not odd:
+                stat_recip(k_next)
+                g_quant((n + 4) // 2)

@@ -21,7 +21,8 @@ MROWS = 256
 
 FLOPS = 2 * SERIES * MROWS * D * N
 
-LAG = 2
+LAG = 3
+EV = 640
 
 
 def tile_segmerging_kernel(tc, x, gamma, beta, W, b, win_size, grad_out, out):
@@ -45,8 +46,8 @@ def tile_segmerging_kernel(tc, x, gamma, beta, W, b, win_size, grad_out, out):
         ypool = ctx.enter_context(tc.tile_pool(name="ypool", bufs=14))
         gpool = ctx.enter_context(tc.tile_pool(name="gpool", bufs=4))
         qpool = ctx.enter_context(tc.tile_pool(name="qpool", bufs=3))
-        azpool = ctx.enter_context(tc.tile_pool(name="azpool", bufs=7))
-        tpool = ctx.enter_context(tc.tile_pool(name="tpool", bufs=5))
+        azpool = ctx.enter_context(tc.tile_pool(name="azpool", bufs=8))
+        tpool = ctx.enter_context(tc.tile_pool(name="tpool", bufs=6))
         jpool = ctx.enter_context(tc.tile_pool(name="jpool", bufs=2))
         small = ctx.enter_context(tc.tile_pool(name="small", bufs=8))
         tp_ps = ctx.enter_context(tc.psum_pool(name="tp_ps", bufs=2))
@@ -301,11 +302,20 @@ def tile_segmerging_kernel(tc, x, gamma, beta, W, b, win_size, grad_out, out):
                 nc.gpsimd.tensor_scalar(out=ts[n][:], in0=ys[n][:], scalar1=p["nb"][:],
                                         scalar2=p["nc"][:], op0=ALU.mult, op1=ALU.add)
 
+        def pass_e_g(n):
+            if n <= 0 or n >= NT:
+                return
+            az = azs[n]
+            nc.gpsimd.tensor_tensor(out=az[:, EV:N], in0=az[:, EV:N], in1=ts[n][:, EV:N],
+                                    op=ALU.subtract)
+
         def pass_e(n):
             if n < 0 or n >= NT:
                 return
             az = azs[n]
-            nc.vector.tensor_tensor(out=az[:], in0=az[:], in1=ts[n][:], op=ALU.subtract)
+            w = N if n == 0 else EV
+            nc.vector.tensor_tensor(out=az[:, 0:w], in0=az[:, 0:w], in1=ts[n][:, 0:w],
+                                    op=ALU.subtract)
             if n == 0:
                 nc.vector.tensor_tensor(out=cls[0:32, :], in0=az[0:32, 0:D], in1=az[0:32, D:N],
                                         op=ALU.add)
@@ -372,32 +382,30 @@ def tile_segmerging_kernel(tc, x, gamma, beta, W, b, win_size, grad_out, out):
                 load((n + 9) // 2)
                 g_transpose((n + 5) // 2)
             mx(n + 2)
+            pass_t(n - 2, "s")
             if odd:
                 stat_negmu(k_stat)
                 stat_unit(k_stat, 2)
                 stat_unit(k_stat, 3)
             else:
-                if n == 0:
-                    stat_sqrt(1)
-                g_copy((n + 4) // 2, "s")
+                stat_sqrt(k_next)
                 stat_unit(k_stat, 0)
                 stat_unit(k_stat, 1)
+            pass_e_g(n - LAG)
             if 0 < n < NT:
                 a_half(n, 0)
-            coef_nb(n - 1)
-            if 0 < n < NT:
                 a_half(n, 1)
-            coef_nc(n - 1)
-            pass_t(n - 1, "s")
-            if odd:
-                stat_sqrt(k_stat)
+            if not odd:
+                g_copy((n + 4) // 2, "v")
             pass_e(n - LAG)
+            coef_nb(n - 1)
             if n < NT:
                 coef_ne1(n)
             if odd:
                 stat_r2n((n + 1) // 2)
             if n < NT:
                 pass_b(n)
+            coef_nc(n - 1)
             if not odd:
                 stat_recip(k_next)
                 g_quant((n + 4) // 2)

@@ -21,8 +21,8 @@ MROWS = 256
 
 FLOPS = 2 * SERIES * MROWS * D * N
 
-LAG = 3
-EV = 640
+LAG = 2
+T_ON_VECTOR = (11, 22, 32)
 
 
 def tile_segmerging_kernel(tc, x, gamma, beta, W, b, win_size, grad_out, out):
@@ -43,8 +43,8 @@ def tile_segmerging_kernel(tc, x, gamma, beta, W, b, win_size, grad_out, out):
 
     with ExitStack() as ctx:
         const = ctx.enter_context(tc.tile_pool(name="const", bufs=1))
-        ypool = ctx.enter_context(tc.tile_pool(name="ypool", bufs=14))
-        gpool = ctx.enter_context(tc.tile_pool(name="gpool", bufs=4))
+        ypool = ctx.enter_context(tc.tile_pool(name="ypool", bufs=18))
+        gpool = ctx.enter_context(tc.tile_pool(name="gpool", bufs=5))
         qpool = ctx.enter_context(tc.tile_pool(name="qpool", bufs=3))
         azpool = ctx.enter_context(tc.tile_pool(name="azpool", bufs=8))
         tpool = ctx.enter_context(tc.tile_pool(name="tpool", bufs=6))
@@ -52,7 +52,6 @@ def tile_segmerging_kernel(tc, x, gamma, beta, W, b, win_size, grad_out, out):
         small = ctx.enter_context(tc.tile_pool(name="small", bufs=8))
         tp_ps = ctx.enter_context(tc.psum_pool(name="tp_ps", bufs=2))
         dyn_ps = ctx.enter_context(tc.psum_pool(name="dyn_ps", bufs=3))
-        ctx.enter_context(tc.manual_schedule())
 
         g_raw = {}
         ys = {}
@@ -299,23 +298,14 @@ def tile_segmerging_kernel(tc, x, gamma, beta, W, b, win_size, grad_out, out):
                 nc.scalar.activation(out=ts[n][:], in_=ys[n][:], func=ACT.Identity,
                                      scale=p["nb"][:], bias=p["nc"][:])
             else:
-                nc.gpsimd.tensor_scalar(out=ts[n][:], in0=ys[n][:], scalar1=p["nb"][:],
+                nc.vector.tensor_scalar(out=ts[n][:], in0=ys[n][:], scalar1=p["nb"][:],
                                         scalar2=p["nc"][:], op0=ALU.mult, op1=ALU.add)
-
-        def pass_e_g(n):
-            if n <= 0 or n >= NT:
-                return
-            az = azs[n]
-            nc.gpsimd.tensor_tensor(out=az[:, EV:N], in0=az[:, EV:N], in1=ts[n][:, EV:N],
-                                    op=ALU.subtract)
 
         def pass_e(n):
             if n < 0 or n >= NT:
                 return
             az = azs[n]
-            w = N if n == 0 else EV
-            nc.vector.tensor_tensor(out=az[:, 0:w], in0=az[:, 0:w], in1=ts[n][:, 0:w],
-                                    op=ALU.subtract)
+            nc.vector.tensor_tensor(out=az[:], in0=az[:], in1=ts[n][:], op=ALU.subtract)
             if n == 0:
                 nc.vector.tensor_tensor(out=cls[0:32, :], in0=az[0:32, 0:D], in1=az[0:32, D:N],
                                         op=ALU.add)
@@ -330,8 +320,8 @@ def tile_segmerging_kernel(tc, x, gamma, beta, W, b, win_size, grad_out, out):
         nc.vector.memset(gamma_row[:], 0.0)
         nc.vector.memset(ones[:], 1.0)
         nc.scalar.dma_start(out=gamma_row[0:1, :], in_=gamma.unsqueeze(0))
-        load_w(0)
         load(0)
+        load_w(0)
         load_w(1)
         for k in range(1, 5):
             load(k)
@@ -339,7 +329,7 @@ def tile_segmerging_kernel(tc, x, gamma, beta, W, b, win_size, grad_out, out):
             gp = dyn_ps.tile([P, 512], F32, name="acc%d" % hf)
             nc.tensor.matmul(out=gp[:], lhsT=ones[:], rhs=gamma_row[:, 512 * hf:512 * hf + 512],
                              start=True, stop=True)
-            nc.scalar.copy(out=gamma_bc[:, 512 * hf:512 * hf + 512], in_=gp[:])
+            nc.vector.tensor_copy(out=gamma_bc[:, 512 * hf:512 * hf + 512], in_=gp[:])
         g_transpose(0)
         g_copy(0, "v")
         g_quant(0)
@@ -382,30 +372,32 @@ def tile_segmerging_kernel(tc, x, gamma, beta, W, b, win_size, grad_out, out):
                 load((n + 9) // 2)
                 g_transpose((n + 5) // 2)
             mx(n + 2)
-            pass_t(n - 2, "s")
             if odd:
                 stat_negmu(k_stat)
                 stat_unit(k_stat, 2)
                 stat_unit(k_stat, 3)
             else:
-                stat_sqrt(k_next)
+                if n == 0:
+                    stat_sqrt(1)
+                g_copy((n + 4) // 2, "s")
                 stat_unit(k_stat, 0)
                 stat_unit(k_stat, 1)
-            pass_e_g(n - LAG)
             if 0 < n < NT:
                 a_half(n, 0)
-                a_half(n, 1)
-            if not odd:
-                g_copy((n + 4) // 2, "v")
-            pass_e(n - LAG)
             coef_nb(n - 1)
+            if 0 < n < NT:
+                a_half(n, 1)
+            coef_nc(n - 1)
+            pass_t(n - 1, "v" if (n - 1) in T_ON_VECTOR else "s")
+            if odd:
+                stat_sqrt(k_stat)
+            pass_e(n - LAG)
             if n < NT:
                 coef_ne1(n)
             if odd:
                 stat_r2n((n + 1) // 2)
             if n < NT:
                 pass_b(n)
-            coef_nc(n - 1)
             if not odd:
                 stat_recip(k_next)
                 g_quant((n + 4) // 2)

@@ -14,15 +14,13 @@ ACT = mybir.ActivationFunctionType
 
 P = 128
 D = 512
-N = 1024
+N = 2 * D
 SERIES = 16
-EPS = 1e-5
 MROWS = 256
+EPS = 1e-5
+LAG = 2
 
 FLOPS = 2 * SERIES * MROWS * D * N
-
-LAG = 2
-T_ON_VECTOR = (11, 22, 32)
 
 
 def tile_segmerging_kernel(tc, x, gamma, beta, W, b, win_size, grad_out, out):
@@ -31,9 +29,13 @@ def tile_segmerging_kernel(tc, x, gamma, beta, W, b, win_size, grad_out, out):
     g3 = grad_out.rearrange("a b m d -> (a b) m d")
     o3 = out.rearrange("a b n d -> (a b) n d")
 
-    groups = [[0]] + [[2 * k - 1, 2 * k] for k in range(1, SERIES + 1)]
+    tiles = [None]
+    for s in range(SERIES):
+        tiles.extend([(s, 1), (s, P)])
+    NT = len(tiles)
+    tiles[NT - 3], tiles[NT - 2] = tiles[NT - 2], tiles[NT - 3]
+    groups = [[0]] + [[n, n + 1] for n in range(1, NT, 2)]
     NG = len(groups)
-    NT = 2 * SERIES + 1
 
     def grp_of(n):
         return (n + 1) // 2
@@ -41,17 +43,23 @@ def tile_segmerging_kernel(tc, x, gamma, beta, W, b, win_size, grad_out, out):
     def idx_in_grp(n):
         return 0 if n == 0 else (n - 1) % 2
 
+    def merged_rows(dram3, n):
+        s, m0 = tiles[n]
+        r0 = 2 * m0 - 1
+        return dram3[s, r0:r0 + 2 * P, :]
+
     with ExitStack() as ctx:
         const = ctx.enter_context(tc.tile_pool(name="const", bufs=1))
-        ypool = ctx.enter_context(tc.tile_pool(name="ypool", bufs=18))
-        gpool = ctx.enter_context(tc.tile_pool(name="gpool", bufs=5))
+        ypool = ctx.enter_context(tc.tile_pool(name="ypool", bufs=14))
+        gpool = ctx.enter_context(tc.tile_pool(name="gpool", bufs=4))
         qpool = ctx.enter_context(tc.tile_pool(name="qpool", bufs=3))
-        azpool = ctx.enter_context(tc.tile_pool(name="azpool", bufs=8))
-        tpool = ctx.enter_context(tc.tile_pool(name="tpool", bufs=6))
+        azpool = ctx.enter_context(tc.tile_pool(name="azpool", bufs=7))
+        tpool = ctx.enter_context(tc.tile_pool(name="tpool", bufs=5))
         jpool = ctx.enter_context(tc.tile_pool(name="jpool", bufs=2))
         small = ctx.enter_context(tc.tile_pool(name="small", bufs=8))
         tp_ps = ctx.enter_context(tc.psum_pool(name="tp_ps", bufs=2))
         dyn_ps = ctx.enter_context(tc.psum_pool(name="dyn_ps", bufs=3))
+        ctx.enter_context(tc.manual_schedule())
 
         g_raw = {}
         ys = {}
@@ -84,7 +92,7 @@ def tile_segmerging_kernel(tc, x, gamma, beta, W, b, win_size, grad_out, out):
         def load_w(hf):
             nc.sync.dma_start(
                 out=w_raw[:, 4 * hf:4 * hf + 4, :],
-                in_=W[512 * hf:512 * hf + 512, :].rearrange("(a p) k -> p a k", p=P),
+                in_=W[D * hf:D * hf + D, :].rearrange("(a p) k -> p a k", p=P),
             )
 
         def load(k):
@@ -102,34 +110,30 @@ def tile_segmerging_kernel(tc, x, gamma, beta, W, b, win_size, grad_out, out):
                     nc.sync.dma_start(out=y[0:SERIES, 0:D], in_=x3[:, 0, :])
                     nc.sync.dma_start(out=y[0:SERIES, D:N], in_=x3[:, 0, :])
                 else:
-                    m0 = 1 + 127 * h
-                    r0 = 2 * m0 - 1
-                    nc.sync.dma_start(out=gr[:, h, :], in_=g3[k - 1, m0:m0 + P, :])
-                    nc.sync.dma_start(
-                        out=y[:],
-                        in_=x3[k - 1, r0:r0 + 2 * P, :].rearrange("(p r) c -> p (r c)", r=2),
-                    )
+                    s, m0 = tiles[n]
+                    nc.sync.dma_start(out=gr[:, h, :], in_=g3[s, m0:m0 + P, :])
+                    nc.sync.dma_start(out=y[:],
+                                      in_=merged_rows(x3, n).rearrange("(p r) c -> p (r c)", r=2))
 
-        def w_transpose(q):
+        def transpose_words(dst, src_bf16):
+            words = src_bf16.bitcast(F32)
+            for u in range(2):
+                nc.tensor.transpose(dst[:, u, :], words[:, P * u:P * u + P], ident[:])
+
+        def w_turn(q):
             wt = tp_ps.tile([P, 2, 2, P], F32, name="wt", tag="tp")
             for a2 in range(2):
-                src = w_raw[:, 2 * q + a2, :].bitcast(F32)
-                for u in range(2):
-                    nc.tensor.transpose(wt[:, a2, u, :], src[:, P * u:P * u + P], ident[:])
-            return wt
-
-        def w_copy(q, wt, eng):
-            dst = w_grp32[:, 256 * q:256 * q + 256, :].rearrange("p (a j) u -> p a j u", a=2)
-            if eng == "v":
-                nc.vector.tensor_copy(out=dst, in_=wt[:].rearrange("p a u j -> p a j u"))
-            else:
-                nc.scalar.copy(out=dst, in_=wt[:].rearrange("p a u j -> p a j u"))
+                transpose_words(wt[:, a2, :, :], w_raw[:, 2 * q + a2, :])
+            nc.vector.tensor_copy(
+                out=w_grp32[:, 256 * q:256 * q + 256, :].rearrange("p (a j) u -> p a j u", a=2),
+                in_=wt[:].rearrange("p a u j -> p a j u"),
+            )
 
         def w_quant(hf):
             nc.vector.quantize_mx(
-                out=w_codes[:, 512 * hf:512 * hf + 512].bitcast(E4X4),
-                scales=w_scales[:, 512 * hf:512 * hf + 512],
-                in_=w_grp[:, 512 * hf:512 * hf + 512, :].rearrange("p j t -> p (j t)"),
+                out=w_codes[:, D * hf:D * hf + D].bitcast(E4X4),
+                scales=w_scales[:, D * hf:D * hf + D],
+                in_=w_grp[:, D * hf:D * hf + D, :].rearrange("p j t -> p (j t)"),
             )
 
         def g_transpose(k):
@@ -138,11 +142,9 @@ def tile_segmerging_kernel(tc, x, gamma, beta, W, b, win_size, grad_out, out):
             gt = tp_ps.tile([P, 2, 2, P], F32, name="gt", tag="tp")
             gts[k] = gt
             for h in range(len(groups[k])):
-                src = g_raw[k][:, h, :].bitcast(F32)
-                for u in range(2):
-                    nc.tensor.transpose(gt[:, h, u, :], src[:, P * u:P * u + P], ident[:])
+                transpose_words(gt[:, h, :, :], g_raw[k][:, h, :])
 
-        def g_copy(k, eng):
+        def g_copy(k, on_vector):
             if k >= NG:
                 return
             m = len(groups[k])
@@ -150,7 +152,7 @@ def tile_segmerging_kernel(tc, x, gamma, beta, W, b, win_size, grad_out, out):
             g_grp[k] = gg
             dst = gg[:].bitcast(F32)[:, 0:P * m, :].rearrange("p (h t) u -> p h t u", h=m)
             src = gts[k][:, 0:m, :, :].rearrange("p h u t -> p h t u")
-            if eng == "v":
+            if on_vector:
                 nc.vector.tensor_copy(out=dst, in_=src)
             else:
                 nc.scalar.copy(out=dst, in_=src)
@@ -168,105 +170,96 @@ def tile_segmerging_kernel(tc, x, gamma, beta, W, b, win_size, grad_out, out):
                 in_=g_grp[k][:, 0:P * m, :].rearrange("p t k -> p (t k)"),
             )
 
-        def stat_unit(k, r):
-            if k >= NG:
+        def stat_sum(k, h):
+            if k >= NG or h >= len(groups[k]):
                 return
-            m = len(groups[k])
-            if r == 0:
+            if h == 0:
                 st[k] = {}
                 for nm in ("sy", "negmu", "ssq", "sd", "rstd", "r2n"):
                     st[k][nm] = small.tile([P, 2], F32, name=nm)
-            s = st[k]
-            h = r % 2
-            if h < m:
-                junk = jpool.tile([P, N], BF16, name="junk")
-                y = ys[groups[k][h]]
-                if r < 2:
-                    nc.scalar.activation(out=junk[:], in_=y[:], func=ACT.Identity,
-                                         accum_out=s["sy"][:, h:h + 1])
-                else:
-                    nc.scalar.activation(out=junk[:], in_=y[:], func=ACT.Square,
-                                         bias=s["negmu"][:, h:h + 1], scale=1.0,
-                                         accum_out=s["ssq"][:, h:h + 1])
+            junk = jpool.tile([P, N], BF16, name="junk")
+            nc.scalar.activation(out=junk[:], in_=ys[groups[k][h]][:], func=ACT.Identity,
+                                 accum_out=st[k]["sy"][:, h:h + 1])
 
         def stat_negmu(k):
             if k >= NG:
                 return
             m = len(groups[k])
-            s = st[k]
-            nc.scalar.mul(out=s["negmu"][:, 0:m], in_=s["sy"][:, 0:m], mul=-1.0 / N)
+            nc.scalar.mul(out=st[k]["negmu"][:, 0:m], in_=st[k]["sy"][:, 0:m], mul=-1.0 / N)
+
+        def stat_square(k, h):
+            if k >= NG or h >= len(groups[k]):
+                return
+            junk = jpool.tile([P, N], BF16, name="junk")
+            nc.scalar.activation(out=junk[:], in_=ys[groups[k][h]][:], func=ACT.Square,
+                                 bias=st[k]["negmu"][:, h:h + 1], scale=1.0,
+                                 accum_out=st[k]["ssq"][:, h:h + 1])
 
         def stat_sqrt(k):
             if k >= NG:
                 return
             m = len(groups[k])
-            s = st[k]
-            nc.scalar.activation(out=s["sd"][:, 0:m], in_=s["ssq"][:, 0:m], func=ACT.Sqrt,
+            nc.scalar.activation(out=st[k]["sd"][:, 0:m], in_=st[k]["ssq"][:, 0:m], func=ACT.Sqrt,
                                  bias=eps_col[:], scale=1.0 / N)
 
         def stat_recip(k):
             if k >= NG:
                 return
             m = len(groups[k])
-            s = st[k]
-            nc.vector.reciprocal(out=s["rstd"][:, 0:m], in_=s["sd"][:, 0:m])
+            nc.vector.reciprocal(out=st[k]["rstd"][:, 0:m], in_=st[k]["sd"][:, 0:m])
 
         def stat_r2n(k):
             if k >= NG:
                 return
             m = len(groups[k])
-            s = st[k]
             nc.vector.scalar_tensor_tensor(
-                out=s["r2n"][:, 0:m], in0=s["rstd"][:, 0:m], scalar=1.0 / N,
-                in1=s["rstd"][:, 0:m], op0=ALU.mult, op1=ALU.mult)
-
-        def mx_half(n, hf):
-            k = grp_of(n)
-            h = idx_in_grp(n)
-            codes, scales = g_q[k]
-            a = dyn_ps.tile([P, 512], F32, name="acc%d" % hf)
-            nc.tensor.matmul_mx(
-                out=a[:],
-                lhsT=codes[:, P * h:P * h + P].bitcast(E5X4),
-                lhsT_scale=scales[:, P * h:P * h + P],
-                rhs=w_codes[:, 512 * hf:512 * hf + 512].bitcast(E4X4),
-                rhs_scale=w_scales[:, 512 * hf:512 * hf + 512],
-                start=True, stop=True,
-            )
-            acc[(n, hf)] = a
+                out=st[k]["r2n"][:, 0:m], in0=st[k]["rstd"][:, 0:m], scalar=1.0 / N,
+                in1=st[k]["rstd"][:, 0:m], op0=ALU.mult, op1=ALU.mult)
 
         def mx(n):
             if n >= NT:
                 return
-            mx_half(n, 0)
-            mx_half(n, 1)
+            h = idx_in_grp(n)
+            codes, scales = g_q[grp_of(n)]
+            for hf in range(2):
+                a = dyn_ps.tile([P, D], F32, name="acc%d" % hf)
+                nc.tensor.matmul_mx(
+                    out=a[:],
+                    lhsT=codes[:, P * h:P * h + P].bitcast(E5X4),
+                    lhsT_scale=scales[:, P * h:P * h + P],
+                    rhs=w_codes[:, D * hf:D * hf + D].bitcast(E4X4),
+                    rhs_scale=w_scales[:, D * hf:D * hf + D],
+                    start=True, stop=True,
+                )
+                acc[(n, hf)] = a
 
         def a_half(n, hf):
-            s = st[grp_of(n)]
-            h = idx_in_grp(n)
+            if n >= NT:
+                return
             if hf == 0:
                 azs[n] = azpool.tile([P, N], F32, name="az")
                 per[n] = {}
                 for nm, w in (("s1", 2), ("dot", 1), ("ne1", 1), ("nb", 1), ("nc", 1)):
                     per[n][nm] = small.tile([P, w], F32, name=nm)
+            h = idx_in_grp(n)
             nc.vector.scalar_tensor_tensor(
-                out=azs[n][:, 512 * hf:512 * hf + 512], in0=acc[(n, hf)][:],
-                scalar=s["rstd"][:, h:h + 1], in1=gamma_bc[:, 512 * hf:512 * hf + 512],
+                out=azs[n][:, D * hf:D * hf + D], in0=acc[(n, hf)][:],
+                scalar=st[grp_of(n)]["rstd"][:, h:h + 1], in1=gamma_bc[:, D * hf:D * hf + D],
                 op0=ALU.mult, op1=ALU.mult, accum_out=per[n]["s1"][:, hf:hf + 1],
             )
 
         def pass_b(n):
-            s = st[grp_of(n)]
+            if n >= NT:
+                return
             h = idx_in_grp(n)
-            t = tpool.tile([P, N], F32, name="t")
-            ts[n] = t
+            ts[n] = tpool.tile([P, N], F32, name="t")
             nc.vector.scalar_tensor_tensor(
-                out=t[:], in0=ys[n][:], scalar=s["negmu"][:, h:h + 1], in1=azs[n][:],
-                op0=ALU.add, op1=ALU.mult, accum_out=per[n]["dot"][:],
+                out=ts[n][:], in0=ys[n][:], scalar=st[grp_of(n)]["negmu"][:, h:h + 1],
+                in1=azs[n][:], op0=ALU.add, op1=ALU.mult, accum_out=per[n]["dot"][:],
             )
 
         def coef_ne1(n):
-            if n < 0 or n >= NT:
+            if n >= NT:
                 return
             p = per[n]
             nc.vector.tensor_scalar(out=p["ne1"][:], in0=p["s1"][:, 0:1], scalar1=p["s1"][:, 1:2],
@@ -275,47 +268,46 @@ def tile_segmerging_kernel(tc, x, gamma, beta, W, b, win_size, grad_out, out):
         def coef_nb(n):
             if n < 0 or n >= NT:
                 return
-            s = st[grp_of(n)]
             h = idx_in_grp(n)
-            p = per[n]
-            nc.vector.tensor_scalar(out=p["nb"][:], in0=p["dot"][:], scalar1=s["r2n"][:, h:h + 1],
-                                    scalar2=None, op0=ALU.mult)
+            nc.vector.tensor_scalar(out=per[n]["nb"][:], in0=per[n]["dot"][:],
+                                    scalar1=st[grp_of(n)]["r2n"][:, h:h + 1], scalar2=None,
+                                    op0=ALU.mult)
 
         def coef_nc(n):
             if n < 0 or n >= NT:
                 return
-            s = st[grp_of(n)]
             h = idx_in_grp(n)
-            p = per[n]
-            nc.vector.tensor_scalar(out=p["nc"][:], in0=p["nb"][:], scalar1=s["negmu"][:, h:h + 1],
-                                    scalar2=p["ne1"][:], op0=ALU.mult, op1=ALU.add)
+            nc.vector.tensor_scalar(out=per[n]["nc"][:], in0=per[n]["nb"][:],
+                                    scalar1=st[grp_of(n)]["negmu"][:, h:h + 1],
+                                    scalar2=per[n]["ne1"][:], op0=ALU.mult, op1=ALU.add)
 
-        def pass_t(n, eng):
+        def pass_t(n):
             if n < 0 or n >= NT:
                 return
-            p = per[n]
-            if eng == "s":
-                nc.scalar.activation(out=ts[n][:], in_=ys[n][:], func=ACT.Identity,
-                                     scale=p["nb"][:], bias=p["nc"][:])
-            else:
-                nc.vector.tensor_scalar(out=ts[n][:], in0=ys[n][:], scalar1=p["nb"][:],
-                                        scalar2=p["nc"][:], op0=ALU.mult, op1=ALU.add)
+            nc.scalar.activation(out=ts[n][:], in_=ys[n][:], func=ACT.Identity,
+                                 scale=per[n]["nb"][:], bias=per[n]["nc"][:])
 
         def pass_e(n):
             if n < 0 or n >= NT:
                 return
             az = azs[n]
-            nc.vector.tensor_tensor(out=az[:], in0=az[:], in1=ts[n][:], op=ALU.subtract)
+            t = ts[n]
+            if n == NT - 1:
+                rows = merged_rows(o3, n).rearrange("(p r) c -> p r c", r=2)
+                for hf in range(2):
+                    cols = slice(D * hf, D * hf + D)
+                    nc.vector.tensor_tensor(out=az[:, cols], in0=az[:, cols], in1=t[:, cols],
+                                            op=ALU.subtract)
+                    nc.sync.dma_start(out=rows[:, hf, :], in_=az[:, cols])
+                return
+            nc.vector.tensor_tensor(out=az[:], in0=az[:], in1=t[:], op=ALU.subtract)
             if n == 0:
                 nc.vector.tensor_tensor(out=cls[0:32, :], in0=az[0:32, 0:D], in1=az[0:32, D:N],
                                         op=ALU.add)
                 nc.sync.dma_start(out=o3[:, 0, :], in_=cls[0:SERIES, :])
             else:
-                r0 = 2 * (1 + 127 * idx_in_grp(n)) - 1
-                nc.sync.dma_start(
-                    out=o3[grp_of(n) - 1, r0:r0 + 2 * P, :].rearrange("(p r) c -> p (r c)", r=2),
-                    in_=az[:],
-                )
+                nc.sync.dma_start(out=merged_rows(o3, n).rearrange("(p r) c -> p (r c)", r=2),
+                                  in_=az[:])
 
         nc.vector.memset(gamma_row[:], 0.0)
         nc.vector.memset(ones[:], 1.0)
@@ -326,43 +318,38 @@ def tile_segmerging_kernel(tc, x, gamma, beta, W, b, win_size, grad_out, out):
         for k in range(1, 5):
             load(k)
         for hf in range(2):
-            gp = dyn_ps.tile([P, 512], F32, name="acc%d" % hf)
-            nc.tensor.matmul(out=gp[:], lhsT=ones[:], rhs=gamma_row[:, 512 * hf:512 * hf + 512],
+            gp = dyn_ps.tile([P, D], F32, name="acc%d" % hf)
+            nc.tensor.matmul(out=gp[:], lhsT=ones[:], rhs=gamma_row[:, D * hf:D * hf + D],
                              start=True, stop=True)
-            nc.vector.tensor_copy(out=gamma_bc[:, 512 * hf:512 * hf + 512], in_=gp[:])
+            nc.vector.tensor_copy(out=gamma_bc[:, D * hf:D * hf + D], in_=gp[:])
         g_transpose(0)
-        g_copy(0, "v")
+        g_copy(0, True)
         g_quant(0)
-        stat_unit(0, 0)
-        wt0 = w_transpose(0)
-        w_copy(0, wt0, "v")
-        wt1 = w_transpose(1)
-        w_copy(1, wt1, "s")
+        stat_sum(0, 0)
         stat_negmu(0)
-        w_quant(0)
-        stat_unit(0, 2)
-        wt2 = w_transpose(2)
-        w_copy(2, wt2, "v")
-        wt3 = w_transpose(3)
-        w_copy(3, wt3, "s")
+        stat_square(0, 0)
         stat_sqrt(0)
+        w_turn(0)
+        w_turn(1)
+        w_quant(0)
         stat_recip(0)
-        mx_half(0, 0)
+        w_turn(2)
+        w_turn(3)
         w_quant(1)
         stat_r2n(0)
-        a_half(0, 0)
-        mx_half(0, 1)
-        a_half(0, 1)
         g_transpose(1)
-        stat_unit(1, 0)
-        stat_unit(1, 1)
-        g_copy(1, "s")
-        stat_negmu(1)
+        g_copy(1, True)
         g_quant(1)
+        mx(0)
         mx(1)
         g_transpose(2)
-        stat_unit(1, 2)
-        stat_unit(1, 3)
+        a_half(0, 0)
+        a_half(0, 1)
+        stat_sum(1, 0)
+        stat_sum(1, 1)
+        stat_negmu(1)
+        stat_square(1, 0)
+        stat_square(1, 1)
 
         for n in range(NT + LAG):
             odd = n % 2 == 1
@@ -374,30 +361,28 @@ def tile_segmerging_kernel(tc, x, gamma, beta, W, b, win_size, grad_out, out):
             mx(n + 2)
             if odd:
                 stat_negmu(k_stat)
-                stat_unit(k_stat, 2)
-                stat_unit(k_stat, 3)
+                stat_square(k_stat, 0)
+                stat_square(k_stat, 1)
             else:
                 if n == 0:
                     stat_sqrt(1)
-                g_copy((n + 4) // 2, "s")
-                stat_unit(k_stat, 0)
-                stat_unit(k_stat, 1)
-            if 0 < n < NT:
+                g_copy((n + 4) // 2, False)
+                stat_sum(k_stat, 0)
+                stat_sum(k_stat, 1)
+            if n > 0:
                 a_half(n, 0)
             coef_nb(n - 1)
-            if 0 < n < NT:
+            if n > 0:
                 a_half(n, 1)
             coef_nc(n - 1)
-            pass_t(n - 1, "v" if (n - 1) in T_ON_VECTOR else "s")
+            pass_t(n - 1)
             if odd:
                 stat_sqrt(k_stat)
             pass_e(n - LAG)
-            if n < NT:
-                coef_ne1(n)
+            coef_ne1(n)
             if odd:
                 stat_r2n((n + 1) // 2)
-            if n < NT:
-                pass_b(n)
+            pass_b(n)
             if not odd:
                 stat_recip(k_next)
                 g_quant((n + 4) // 2)

@@ -95,12 +95,12 @@ def tile_segmerging_kernel(tc, x, gamma, beta, W, b, win_size, grad_out, out):
                 in_=W[D * hf:D * hf + D, :].rearrange("(a p) k -> p a k", p=P),
             )
 
-        def load(k):
-            if k >= NG:
+        def load(gi):
+            if gi >= NG:
                 return
             gr = gpool.tile([P, 2, D], BF16, name="g_raw")
-            g_raw[k] = gr
-            for h, n in enumerate(groups[k]):
+            g_raw[gi] = gr
+            for h, n in enumerate(groups[gi]):
                 y = ypool.tile([P, N], BF16, name="y")
                 ys[n] = y
                 if n == 0:
@@ -133,88 +133,88 @@ def tile_segmerging_kernel(tc, x, gamma, beta, W, b, win_size, grad_out, out):
             nc.vector.quantize_mx(
                 out=w_codes[:, D * hf:D * hf + D].bitcast(E4X4),
                 scales=w_scales[:, D * hf:D * hf + D],
-                in_=w_grp[:, D * hf:D * hf + D, :].rearrange("p j t -> p (j t)"),
+                in_=w_grp[:, D * hf:D * hf + D, :].rearrange("p j v -> p (j v)"),
             )
 
-        def g_transpose(k):
-            if k >= NG:
+        def g_transpose(gi):
+            if gi >= NG:
                 return
             gt = tp_ps.tile([P, 2, 2, P], F32, name="gt", tag="tp")
-            gts[k] = gt
-            for h in range(len(groups[k])):
-                transpose_words(gt[:, h, :, :], g_raw[k][:, h, :])
+            gts[gi] = gt
+            for h in range(len(groups[gi])):
+                transpose_words(gt[:, h, :, :], g_raw[gi][:, h, :])
 
-        def g_copy(k, on_vector):
-            if k >= NG:
+        def g_copy(gi, on_vector):
+            if gi >= NG:
                 return
-            m = len(groups[k])
+            m = len(groups[gi])
             gg = qpool.tile([P, 2 * P, 4], BF16, name="g_grp", align_bytes=64)
-            g_grp[k] = gg
+            g_grp[gi] = gg
             dst = gg[:].bitcast(F32)[:, 0:P * m, :].rearrange("p (h t) u -> p h t u", h=m)
-            src = gts[k][:, 0:m, :, :].rearrange("p h u t -> p h t u")
+            src = gts[gi][:, 0:m, :, :].rearrange("p h u t -> p h t u")
             if on_vector:
                 nc.vector.tensor_copy(out=dst, in_=src)
             else:
                 nc.scalar.copy(out=dst, in_=src)
 
-        def g_quant(k):
-            if k >= NG:
+        def g_quant(gi):
+            if gi >= NG:
                 return
-            m = len(groups[k])
+            m = len(groups[gi])
             codes = qpool.tile([P, 2 * P], U32, name="g_codes", align_bytes=64)
             scales = qpool.tile([P, 2 * P], U8, name="g_scales", align_bytes=64)
-            g_q[k] = (codes, scales)
+            g_q[gi] = (codes, scales)
             nc.vector.quantize_mx(
                 out=codes[:, 0:P * m].bitcast(E5X4),
                 scales=scales[:, 0:P * m],
-                in_=g_grp[k][:, 0:P * m, :].rearrange("p t k -> p (t k)"),
+                in_=g_grp[gi][:, 0:P * m, :].rearrange("p t v -> p (t v)"),
             )
 
-        def stat_sum(k, h):
-            if k >= NG or h >= len(groups[k]):
+        def stat_sum(gi, h):
+            if gi >= NG or h >= len(groups[gi]):
                 return
             if h == 0:
-                st[k] = {}
+                st[gi] = {}
                 for nm in ("sy", "negmu", "ssq", "sd", "rstd", "r2n"):
-                    st[k][nm] = small.tile([P, 2], F32, name=nm)
+                    st[gi][nm] = small.tile([P, 2], F32, name=nm)
             junk = jpool.tile([P, N], BF16, name="junk")
-            nc.scalar.activation(out=junk[:], in_=ys[groups[k][h]][:], func=ACT.Identity,
-                                 accum_out=st[k]["sy"][:, h:h + 1])
+            nc.scalar.activation(out=junk[:], in_=ys[groups[gi][h]][:], func=ACT.Identity,
+                                 accum_out=st[gi]["sy"][:, h:h + 1])
 
-        def stat_negmu(k):
-            if k >= NG:
+        def stat_negmu(gi):
+            if gi >= NG:
                 return
-            m = len(groups[k])
-            nc.scalar.mul(out=st[k]["negmu"][:, 0:m], in_=st[k]["sy"][:, 0:m], mul=-1.0 / N)
+            m = len(groups[gi])
+            nc.scalar.mul(out=st[gi]["negmu"][:, 0:m], in_=st[gi]["sy"][:, 0:m], mul=-1.0 / N)
 
-        def stat_square(k, h):
-            if k >= NG or h >= len(groups[k]):
+        def stat_square(gi, h):
+            if gi >= NG or h >= len(groups[gi]):
                 return
             junk = jpool.tile([P, N], BF16, name="junk")
-            nc.scalar.activation(out=junk[:], in_=ys[groups[k][h]][:], func=ACT.Square,
-                                 bias=st[k]["negmu"][:, h:h + 1], scale=1.0,
-                                 accum_out=st[k]["ssq"][:, h:h + 1])
+            nc.scalar.activation(out=junk[:], in_=ys[groups[gi][h]][:], func=ACT.Square,
+                                 bias=st[gi]["negmu"][:, h:h + 1], scale=1.0,
+                                 accum_out=st[gi]["ssq"][:, h:h + 1])
 
-        def stat_sqrt(k):
-            if k >= NG:
+        def stat_sqrt(gi):
+            if gi >= NG:
                 return
-            m = len(groups[k])
-            nc.scalar.activation(out=st[k]["sd"][:, 0:m], in_=st[k]["ssq"][:, 0:m], func=ACT.Sqrt,
+            m = len(groups[gi])
+            nc.scalar.activation(out=st[gi]["sd"][:, 0:m], in_=st[gi]["ssq"][:, 0:m], func=ACT.Sqrt,
                                  bias=eps_col[:], scale=1.0 / N)
 
-        def stat_recip(k):
-            if k >= NG:
+        def stat_recip(gi):
+            if gi >= NG:
                 return
-            m = len(groups[k])
-            nc.vector.reciprocal(out=st[k]["rstd"][:, 0:m], in_=st[k]["sd"][:, 0:m])
+            m = len(groups[gi])
+            nc.vector.reciprocal(out=st[gi]["rstd"][:, 0:m], in_=st[gi]["sd"][:, 0:m])
 
-        def stat_r2n(k):
-            if k >= NG:
+        def stat_r2n(gi):
+            if gi >= NG:
                 return
-            m = len(groups[k])
+            m = len(groups[gi])
             nc.vector.scalar_tensor_tensor(
-                out=st[k]["r2n"][:, 0:m], in0=st[k]["rstd"][:, 0:m], scalar=1.0 / N,
-                in1=st[k]["rstd"][:, 0:m], op0=ALU.mult, op1=ALU.mult)
+                out=st[gi]["r2n"][:, 0:m], in0=st[gi]["rstd"][:, 0:m], scalar=1.0 / N,
+                in1=st[gi]["rstd"][:, 0:m], op0=ALU.mult, op1=ALU.mult)
 
         def mx(n):
             if n >= NT:
@@ -239,7 +239,7 @@ def tile_segmerging_kernel(tc, x, gamma, beta, W, b, win_size, grad_out, out):
             if hf == 0:
                 azs[n] = azpool.tile([P, N], F32, name="az")
                 per[n] = {}
-                for nm, w in (("s1", 2), ("dot", 1), ("ne1", 1), ("nb", 1), ("nc", 1)):
+                for nm, w in (("s1", 2), ("dot", 1), ("am", 1), ("sl", 1), ("of", 1)):
                     per[n][nm] = small.tile([P, w], F32, name=nm)
             h = idx_in_grp(n)
             nc.vector.scalar_tensor_tensor(
@@ -258,34 +258,34 @@ def tile_segmerging_kernel(tc, x, gamma, beta, W, b, win_size, grad_out, out):
                 in1=azs[n][:], op0=ALU.add, op1=ALU.mult, accum_out=per[n]["dot"][:],
             )
 
-        def coef_ne1(n):
+        def coef_am(n):
             if n >= NT:
                 return
-            p = per[n]
-            nc.vector.tensor_scalar(out=p["ne1"][:], in0=p["s1"][:, 0:1], scalar1=p["s1"][:, 1:2],
+            s1 = per[n]["s1"]
+            nc.vector.tensor_scalar(out=per[n]["am"][:], in0=s1[:, 0:1], scalar1=s1[:, 1:2],
                                     scalar2=1.0 / N, op0=ALU.add, op1=ALU.mult)
 
-        def coef_nb(n):
+        def coef_sl(n):
             if n < 0 or n >= NT:
                 return
             h = idx_in_grp(n)
-            nc.vector.tensor_scalar(out=per[n]["nb"][:], in0=per[n]["dot"][:],
+            nc.vector.tensor_scalar(out=per[n]["sl"][:], in0=per[n]["dot"][:],
                                     scalar1=st[grp_of(n)]["r2n"][:, h:h + 1], scalar2=None,
                                     op0=ALU.mult)
 
-        def coef_nc(n):
+        def coef_of(n):
             if n < 0 or n >= NT:
                 return
             h = idx_in_grp(n)
-            nc.vector.tensor_scalar(out=per[n]["nc"][:], in0=per[n]["nb"][:],
+            nc.vector.tensor_scalar(out=per[n]["of"][:], in0=per[n]["sl"][:],
                                     scalar1=st[grp_of(n)]["negmu"][:, h:h + 1],
-                                    scalar2=per[n]["ne1"][:], op0=ALU.mult, op1=ALU.add)
+                                    scalar2=per[n]["am"][:], op0=ALU.mult, op1=ALU.add)
 
         def pass_t(n):
             if n < 0 or n >= NT:
                 return
             nc.scalar.activation(out=ts[n][:], in_=ys[n][:], func=ACT.Identity,
-                                 scale=per[n]["nb"][:], bias=per[n]["nc"][:])
+                                 scale=per[n]["sl"][:], bias=per[n]["of"][:])
 
         def pass_e(n):
             if n < 0 or n >= NT:
@@ -315,8 +315,8 @@ def tile_segmerging_kernel(tc, x, gamma, beta, W, b, win_size, grad_out, out):
         load(0)
         load_w(0)
         load_w(1)
-        for k in range(1, 5):
-            load(k)
+        for gi in range(1, 5):
+            load(gi)
         for hf in range(2):
             gp = dyn_ps.tile([P, D], F32, name="acc%d" % hf)
             nc.tensor.matmul(out=gp[:], lhsT=ones[:], rhs=gamma_row[:, D * hf:D * hf + D],
@@ -353,36 +353,41 @@ def tile_segmerging_kernel(tc, x, gamma, beta, W, b, win_size, grad_out, out):
 
         for n in range(NT + LAG):
             odd = n % 2 == 1
-            k_stat = 2 + n // 2
-            k_next = (n + 2) // 2
+            gi_stat = 2 + n // 2
+            gi_next = (n + 2) // 2
+            gi_turn = (n + 4) // 2
+            copy_on_vector = gi_turn % 2 == 0
             if odd:
                 load((n + 9) // 2)
                 g_transpose((n + 5) // 2)
             mx(n + 2)
             if odd:
-                stat_negmu(k_stat)
-                stat_square(k_stat, 0)
-                stat_square(k_stat, 1)
+                stat_negmu(gi_stat)
+                stat_square(gi_stat, 0)
+                stat_square(gi_stat, 1)
             else:
                 if n == 0:
                     stat_sqrt(1)
-                g_copy((n + 4) // 2, False)
-                stat_sum(k_stat, 0)
-                stat_sum(k_stat, 1)
+                if not copy_on_vector:
+                    g_copy(gi_turn, False)
+                stat_sum(gi_stat, 0)
+                stat_sum(gi_stat, 1)
             if n > 0:
                 a_half(n, 0)
-            coef_nb(n - 1)
+            coef_sl(n - 1)
             if n > 0:
                 a_half(n, 1)
-            coef_nc(n - 1)
+            coef_of(n - 1)
+            if not odd and copy_on_vector:
+                g_copy(gi_turn, True)
             pass_t(n - 1)
             if odd:
-                stat_sqrt(k_stat)
+                stat_sqrt(gi_stat)
             pass_e(n - LAG)
-            coef_ne1(n)
+            coef_am(n)
             if odd:
                 stat_r2n((n + 1) // 2)
             pass_b(n)
             if not odd:
-                stat_recip(k_next)
-                g_quant((n + 4) // 2)
+                stat_recip(gi_next)
+                g_quant(gi_turn)

@@ -356,7 +356,6 @@ def tile_segmerging_kernel(tc, x, gamma, beta, W, b, win_size, grad_out, out):
             gi_stat = 2 + n // 2
             gi_next = (n + 2) // 2
             gi_turn = (n + 4) // 2
-            copy_on_vector = gi_turn % 2 == 0
             if odd:
                 load((n + 9) // 2)
                 g_transpose((n + 5) // 2)
@@ -368,8 +367,7 @@ def tile_segmerging_kernel(tc, x, gamma, beta, W, b, win_size, grad_out, out):
             else:
                 if n == 0:
                     stat_sqrt(1)
-                if not copy_on_vector:
-                    g_copy(gi_turn, False)
+                g_copy(gi_turn, False)
                 stat_sum(gi_stat, 0)
                 stat_sum(gi_stat, 1)
             if n > 0:
@@ -378,8 +376,6 @@ def tile_segmerging_kernel(tc, x, gamma, beta, W, b, win_size, grad_out, out):
             if n > 0:
                 a_half(n, 1)
             coef_of(n - 1)
-            if not odd and copy_on_vector:
-                g_copy(gi_turn, True)
             pass_t(n - 1)
             if odd:
                 stat_sqrt(gi_stat)

from contextlib import ExitStack

import concourse.mybir as mybir
from concourse.masks import make_identity

F32 = mybir.dt.float32
BF16 = mybir.dt.bfloat16
U32 = mybir.dt.uint32
U8 = mybir.dt.uint8
E4X4 = mybir.dt.float8_e4m3fn_x4
E5X4 = mybir.dt.float8_e5m2_x4
ALU = mybir.AluOpType
ACT = mybir.ActivationFunctionType

P = 128
D = 512
N = 2 * D
SERIES = 16
MROWS = 256
EPS = 1e-5
LAG = 2

FLOPS = 2 * SERIES * MROWS * D * N


def tile_segmerging_kernel(tc, x, gamma, beta, W, b, win_size, grad_out, out):
    nc = tc.nc
    x3 = x.rearrange("a b n d -> (a b) n d")
    g3 = grad_out.rearrange("a b m d -> (a b) m d")
    o3 = out.rearrange("a b n d -> (a b) n d")

    tiles = [None]
    for s in range(SERIES):
        tiles.extend([(s, 1), (s, P)])
    NT = len(tiles)
    tiles[NT - 3], tiles[NT - 2] = tiles[NT - 2], tiles[NT - 3]
    groups = [[0]] + [[n, n + 1] for n in range(1, NT, 2)]
    NG = len(groups)

    def grp_of(n):
        return (n + 1) // 2

    def idx_in_grp(n):
        return 0 if n == 0 else (n - 1) % 2

    def merged_rows(dram3, n):
        s, m0 = tiles[n]
        r0 = 2 * m0 - 1
        return dram3[s, r0:r0 + 2 * P, :]

    with ExitStack() as ctx:
        const = ctx.enter_context(tc.tile_pool(name="const", bufs=1))
        ypool = ctx.enter_context(tc.tile_pool(name="ypool", bufs=14))
        gpool = ctx.enter_context(tc.tile_pool(name="gpool", bufs=4))
        qpool = ctx.enter_context(tc.tile_pool(name="qpool", bufs=3))
        azpool = ctx.enter_context(tc.tile_pool(name="azpool", bufs=7))
        tpool = ctx.enter_context(tc.tile_pool(name="tpool", bufs=5))
        jpool = ctx.enter_context(tc.tile_pool(name="jpool", bufs=2))
        small = ctx.enter_context(tc.tile_pool(name="small", bufs=8))
        tp_ps = ctx.enter_context(tc.psum_pool(name="tp_ps", bufs=2))
        dyn_ps = ctx.enter_context(tc.psum_pool(name="dyn_ps", bufs=3))
        ctx.enter_context(tc.manual_schedule())

        g_raw = {}
        ys = {}
        gts = {}
        g_grp = {}
        g_q = {}
        st = {}
        acc = {}
        azs = {}
        ts = {}
        per = {}

        ident = const.tile([P, P], F32, name="ident")
        make_identity(nc, ident[:])
        eps_col = const.tile([P, 1], F32, name="eps_col")
        nc.vector.memset(eps_col[:], EPS)
        warm = const.tile([P, 1], F32, name="warm")
        nc.scalar.activation(out=warm[:], in_=eps_col[:], func=ACT.Sqrt)

        w_raw = const.tile([P, 8, D], BF16, name="w_raw")
        gamma_row = const.tile([P, N], BF16, name="gamma_row")
        ones = const.tile([P, P], BF16, name="ones")
        gamma_bc = const.tile([P, N], BF16, name="gamma_bc")
        w_grp = const.tile([P, N, 4], BF16, name="w_grp", align_bytes=64)
        w_grp32 = w_grp[:].bitcast(F32)
        w_codes = const.tile([P, N], U32, name="w_codes", align_bytes=64)
        w_scales = const.tile([P, N], U8, name="w_scales", align_bytes=64)
        cls = const.tile([P, D], F32, name="cls")

        def load_w(hf):
            nc.sync.dma_start(
                out=w_raw[:, 4 * hf:4 * hf + 4, :],
                in_=W[D * hf:D * hf + D, :].rearrange("(a p) k -> p a k", p=P),
            )

        def load(gi):
            if gi >= NG:
                return
            gr = gpool.tile([P, 2, D], BF16, name="g_raw")
            g_raw[gi] = gr
            for h, n in enumerate(groups[gi]):
                y = ypool.tile([P, N], BF16, name="y")
                ys[n] = y
                if n == 0:
                    nc.vector.memset(gr[:, 0, :], 0.0)
                    nc.vector.memset(y[:], 0.0)
                    nc.sync.dma_start(out=gr[0:SERIES, 0, :], in_=g3[:, 0, :])
                    nc.sync.dma_start(out=y[0:SERIES, 0:D], in_=x3[:, 0, :])
                    nc.sync.dma_start(out=y[0:SERIES, D:N], in_=x3[:, 0, :])
                else:
                    s, m0 = tiles[n]
                    nc.sync.dma_start(out=gr[:, h, :], in_=g3[s, m0:m0 + P, :])
                    nc.sync.dma_start(out=y[:],
                                      in_=merged_rows(x3, n).rearrange("(p r) c -> p (r c)", r=2))

        def transpose_words(dst, src_bf16):
            words = src_bf16.bitcast(F32)
            for u in range(2):
                nc.tensor.transpose(dst[:, u, :], words[:, P * u:P * u + P], ident[:])

        def w_turn(q):
            wt = tp_ps.tile([P, 2, 2, P], F32, name="wt", tag="tp")
            for a2 in range(2):
                transpose_words(wt[:, a2, :, :], w_raw[:, 2 * q + a2, :])
            nc.vector.tensor_copy(
                out=w_grp32[:, 256 * q:256 * q + 256, :].rearrange("p (a j) u -> p a j u", a=2),
                in_=wt[:].rearrange("p a u j -> p a j u"),
            )

        def w_quant(hf):
            nc.vector.quantize_mx(
                out=w_codes[:, D * hf:D * hf + D].bitcast(E4X4),
                scales=w_scales[:, D * hf:D * hf + D],
                in_=w_grp[:, D * hf:D * hf + D, :].rearrange("p j v -> p (j v)"),
            )

        def g_transpose(gi):
            if gi >= NG:
                return
            gt = tp_ps.tile([P, 2, 2, P], F32, name="gt", tag="tp")
            gts[gi] = gt
            for h in range(len(groups[gi])):
                transpose_words(gt[:, h, :, :], g_raw[gi][:, h, :])

        def g_copy(gi, on_vector):
            if gi >= NG:
                return
            m = len(groups[gi])
            gg = qpool.tile([P, 2 * P, 4], BF16, name="g_grp", align_bytes=64)
            g_grp[gi] = gg
            dst = gg[:].bitcast(F32)[:, 0:P * m, :].rearrange("p (h t) u -> p h t u", h=m)
            src = gts[gi][:, 0:m, :, :].rearrange("p h u t -> p h t u")
            if on_vector:
                nc.vector.tensor_copy(out=dst, in_=src)
            else:
                nc.scalar.copy(out=dst, in_=src)

        def g_quant(gi):
            if gi >= NG:
                return
            m = len(groups[gi])
            codes = qpool.tile([P, 2 * P], U32, name="g_codes", align_bytes=64)
            scales = qpool.tile([P, 2 * P], U8, name="g_scales", align_bytes=64)
            g_q[gi] = (codes, scales)
            nc.vector.quantize_mx(
                out=codes[:, 0:P * m].bitcast(E5X4),
                scales=scales[:, 0:P * m],
                in_=g_grp[gi][:, 0:P * m, :].rearrange("p t v -> p (t v)"),
            )

        def stat_sum(gi, h):
            if gi >= NG or h >= len(groups[gi]):
                return
            if h == 0:
                st[gi] = {}
                for nm in ("sy", "negmu", "ssq", "sd", "rstd", "r2n"):
                    st[gi][nm] = small.tile([P, 2], F32, name=nm)
            junk = jpool.tile([P, N], BF16, name="junk")
            nc.scalar.activation(out=junk[:], in_=ys[groups[gi][h]][:], func=ACT.Identity,
                                 accum_out=st[gi]["sy"][:, h:h + 1])

        def stat_negmu(gi):
            if gi >= NG:
                return
            m = len(groups[gi])
            nc.scalar.mul(out=st[gi]["negmu"][:, 0:m], in_=st[gi]["sy"][:, 0:m], mul=-1.0 / N)

        def stat_square(gi, h):
            if gi >= NG or h >= len(groups[gi]):
                return
            junk = jpool.tile([P, N], BF16, name="junk")
            nc.scalar.activation(out=junk[:], in_=ys[groups[gi][h]][:], func=ACT.Square,
                                 bias=st[gi]["negmu"][:, h:h + 1], scale=1.0,
                                 accum_out=st[gi]["ssq"][:, h:h + 1])

        def stat_sqrt(gi):
            if gi >= NG:
                return
            m = len(groups[gi])
            nc.scalar.activation(out=st[gi]["sd"][:, 0:m], in_=st[gi]["ssq"][:, 0:m], func=ACT.Sqrt,
                                 bias=eps_col[:], scale=1.0 / N)

        def stat_recip(gi):
            if gi >= NG:
                return
            m = len(groups[gi])
            nc.vector.reciprocal(out=st[gi]["rstd"][:, 0:m], in_=st[gi]["sd"][:, 0:m])

        def stat_r2n(gi):
            if gi >= NG:
                return
            m = len(groups[gi])
            nc.vector.scalar_tensor_tensor(
                out=st[gi]["r2n"][:, 0:m], in0=st[gi]["rstd"][:, 0:m], scalar=1.0 / N,
                in1=st[gi]["rstd"][:, 0:m], op0=ALU.mult, op1=ALU.mult)

        def mx(n):
            if n >= NT:
                return
            h = idx_in_grp(n)
            codes, scales = g_q[grp_of(n)]
            for hf in range(2):
                a = dyn_ps.tile([P, D], F32, name="acc%d" % hf)
                nc.tensor.matmul_mx(
                    out=a[:],
                    lhsT=codes[:, P * h:P * h + P].bitcast(E5X4),
                    lhsT_scale=scales[:, P * h:P * h + P],
                    rhs=w_codes[:, D * hf:D * hf + D].bitcast(E4X4),
                    rhs_scale=w_scales[:, D * hf:D * hf + D],
                    start=True, stop=True,
                )
                acc[(n, hf)] = a

        def a_half(n, hf):
            if n >= NT:
                return
            if hf == 0:
                azs[n] = azpool.tile([P, N], F32, name="az")
                per[n] = {}
                for nm, w in (("s1", 2), ("dot", 1), ("am", 1), ("sl", 1), ("of", 1)):
                    per[n][nm] = small.tile([P, w], F32, name=nm)
            h = idx_in_grp(n)
            nc.vector.scalar_tensor_tensor(
                out=azs[n][:, D * hf:D * hf + D], in0=acc[(n, hf)][:],
                scalar=st[grp_of(n)]["rstd"][:, h:h + 1], in1=gamma_bc[:, D * hf:D * hf + D],
                op0=ALU.mult, op1=ALU.mult, accum_out=per[n]["s1"][:, hf:hf + 1],
            )

        def pass_b(n):
            if n >= NT:
                return
            h = idx_in_grp(n)
            ts[n] = tpool.tile([P, N], F32, name="t")
            nc.vector.scalar_tensor_tensor(
                out=ts[n][:], in0=ys[n][:], scalar=st[grp_of(n)]["negmu"][:, h:h + 1],
                in1=azs[n][:], op0=ALU.add, op1=ALU.mult, accum_out=per[n]["dot"][:],
            )

        def coef_am(n):
            if n >= NT:
                return
            s1 = per[n]["s1"]
            nc.vector.tensor_scalar(out=per[n]["am"][:], in0=s1[:, 0:1], scalar1=s1[:, 1:2],
                                    scalar2=1.0 / N, op0=ALU.add, op1=ALU.mult)

        def coef_sl(n):
            if n < 0 or n >= NT:
                return
            h = idx_in_grp(n)
            nc.vector.tensor_scalar(out=per[n]["sl"][:], in0=per[n]["dot"][:],
                                    scalar1=st[grp_of(n)]["r2n"][:, h:h + 1], scalar2=None,
                                    op0=ALU.mult)

        def coef_of(n):
            if n < 0 or n >= NT:
                return
            h = idx_in_grp(n)
            nc.vector.tensor_scalar(out=per[n]["of"][:], in0=per[n]["sl"][:],
                                    scalar1=st[grp_of(n)]["negmu"][:, h:h + 1],
                                    scalar2=per[n]["am"][:], op0=ALU.mult, op1=ALU.add)

        def pass_t(n):
            if n < 0 or n >= NT:
                return
            nc.scalar.activation(out=ts[n][:], in_=ys[n][:], func=ACT.Identity,
                                 scale=per[n]["sl"][:], bias=per[n]["of"][:])

        def pass_e(n):
            if n < 0 or n >= NT:
                return
            az = azs[n]
            t = ts[n]
            if n == NT - 1:
                rows = merged_rows(o3, n).rearrange("(p r) c -> p r c", r=2)
                for hf in range(2):
                    cols = slice(D * hf, D * hf + D)
                    nc.vector.tensor_tensor(out=az[:, cols], in0=az[:, cols], in1=t[:, cols],
                                            op=ALU.subtract)
                    nc.sync.dma_start(out=rows[:, hf, :], in_=az[:, cols])
                return
            nc.vector.tensor_tensor(out=az[:], in0=az[:], in1=t[:], op=ALU.subtract)
            if n == 0:
                nc.vector.tensor_tensor(out=cls[0:32, :], in0=az[0:32, 0:D], in1=az[0:32, D:N],
                                        op=ALU.add)
                nc.sync.dma_start(out=o3[:, 0, :], in_=cls[0:SERIES, :])
            else:
                nc.sync.dma_start(out=merged_rows(o3, n).rearrange("(p r) c -> p (r c)", r=2),
                                  in_=az[:])

        nc.vector.memset(gamma_row[:], 0.0)
        nc.vector.memset(ones[:], 1.0)
        nc.scalar.dma_start(out=gamma_row[0:1, :], in_=gamma.unsqueeze(0))
        load(0)
        load_w(0)
        load_w(1)
        for gi in range(1, 5):
            load(gi)
        for hf in range(2):
            gp = dyn_ps.tile([P, D], F32, name="acc%d" % hf)
            nc.tensor.matmul(out=gp[:], lhsT=ones[:], rhs=gamma_row[:, D * hf:D * hf + D],
                             start=True, stop=True)
            nc.vector.tensor_copy(out=gamma_bc[:, D * hf:D * hf + D], in_=gp[:])
        g_transpose(0)
        g_copy(0, True)
        g_quant(0)
        stat_sum(0, 0)
        stat_negmu(0)
        stat_square(0, 0)
        stat_sqrt(0)
        w_turn(0)
        w_turn(1)
        w_quant(0)
        stat_recip(0)
        w_turn(2)
        w_turn(3)
        w_quant(1)
        stat_r2n(0)
        g_transpose(1)
        g_copy(1, True)
        g_quant(1)
        mx(0)
        mx(1)
        g_transpose(2)
        a_half(0, 0)
        a_half(0, 1)
        stat_sum(1, 0)
        stat_sum(1, 1)
        stat_negmu(1)
        stat_square(1, 0)
        stat_square(1, 1)

        for n in range(NT + LAG):
            odd = n % 2 == 1
            gi_stat = 2 + n // 2
            gi_next = (n + 2) // 2
            gi_turn = (n + 4) // 2
            if odd:
                load((n + 9) // 2)
                g_transpose((n + 5) // 2)
            mx(n + 2)
            if odd:
                stat_negmu(gi_stat)
                stat_square(gi_stat, 0)
                stat_square(gi_stat, 1)
            else:
                if n == 0:
                    stat_sqrt(1)
                g_copy(gi_turn, False)
                stat_sum(gi_stat, 0)
                stat_sum(gi_stat, 1)
            if n > 0:
                a_half(n, 0)
            coef_sl(n - 1)
            if n > 0:
                a_half(n, 1)
            coef_of(n - 1)
            pass_t(n - 1)
            if odd:
                stat_sqrt(gi_stat)
            pass_e(n - LAG)
            coef_am(n)
            if odd:
                stat_r2n((n + 1) // 2)
            pass_b(n)
            if not odd:
                stat_recip(gi_next)
                g_quant(gi_turn)
